import numpy as np
import ml_dtypes


def mxq(x, axis, fmt="e4m3"):
    dtype, down = {"e4m3": (ml_dtypes.float8_e4m3fn, 7), "e5m2": (ml_dtypes.float8_e5m2, 14)}[fmt]
    v = np.moveaxis(np.asarray(x, np.float32).astype(ml_dtypes.bfloat16).astype(np.float64), axis, -1)
    blocks = v.reshape(v.shape[:-1] + (-1, 32))
    amax = np.abs(blocks).max(-1, keepdims=True)
    byte = np.maximum(np.where(amax > 0, np.frexp(amax)[1] - 1 + 127, 0) - down, 1)
    scale = np.exp2(byte - 127.0)
    codes = (blocks / scale).astype(np.float32).astype(dtype).astype(np.float64)
    return np.moveaxis((codes * scale).reshape(v.shape), -1, axis)


WIDE = False


def mx_kscale(k):
    if not WIDE:
        return np.ones(k)
    levels = np.array([10, -10, 5, -5, 0])
    a = np.random.permutation(np.resize(levels, k // 512 * 4)).reshape(k // 512, 4)
    idx = np.arange(k)
    return np.exp2(a[idx // 512, idx % 128 // 32])


BF16 = ml_dtypes.bfloat16


def bf(x):
    return np.asarray(x, np.float32).astype(BF16)


def f64(x):
    return np.asarray(x).astype(np.float64)


S, HID, NH, Q_LORA, KV_LORA, NOPE, ROPE, VDIM, BLK = 512, 2048, 16, 1536, 512, 128, 64, 128, 128
HEAD = NOPE + ROPE
EPS = 1e-6


def blockscale(rows, cols, k, g):
    return bf((np.random.random((rows, cols)) * 0.8 + 0.2) * g / np.sqrt(k))


def dequant(w, s):
    so = np.repeat(s, BLK, axis=0)[: w.shape[0]]
    se = np.repeat(so, BLK, axis=1)[:, : w.shape[1]]
    return w * se


def rmsnorm(x, w):
    var = np.mean(x * x, axis=-1, keepdims=True)
    return x * (1.0 / np.sqrt(var + EPS)) * w


def rotate_half(x):
    h = x.shape[-1] // 2
    return np.concatenate([-x[..., h:], x[..., :h]], axis=-1)


def setup_inputs():
    s, t = mx_kscale(HID), mx_kscale(Q_LORA)
    ang = np.arange(S)[:, None] / (10000.0 ** (np.arange(0, ROPE, 2) / ROPE))[None, :]
    ang = np.concatenate([ang, ang], axis=-1)
    return {"hidden_states": bf(np.random.standard_normal((S, HID)) * s),
            "cos": bf(np.cos(ang)),
            "sin": bf(np.sin(ang)),
            "wq_a": bf(np.random.standard_normal((Q_LORA, HID)) / s[None, :]),
            "sq_a": blockscale(Q_LORA // BLK, HID // BLK, HID, 1.0),
            "wq_b": bf(np.random.standard_normal((NH * HEAD, Q_LORA)) / t[None, :]),
            "sq_b": blockscale(NH * HEAD // BLK, Q_LORA // BLK, Q_LORA, 2.0),
            "q_ln_w": bf((1.0 + 0.1 * np.random.standard_normal(Q_LORA)) * t)}


def reference(hidden_states, cos, sin, wq_a, sq_a, wq_b, sq_b, q_ln_w):
    wa = dequant(f64(wq_a), f64(sq_a))
    lq = mxq(f64(hidden_states), 1, "e4m3") @ mxq(wa, 1, "e4m3").T
    h = rmsnorm(lq, f64(q_ln_w))
    wb = dequant(f64(wq_b), f64(sq_b))
    q = (mxq(h, 1, "e4m3") @ mxq(wb, 1, "e4m3").T).reshape(S, NH, HEAD)
    q_nope, q_pe = q[..., :NOPE], q[..., NOPE:]
    q_rot = q_pe * f64(cos)[:, None, :] + rotate_half(q_pe) * f64(sin)[:, None, :]
    return q_nope, q_rot

@@ -1,0 +1,329 @@
+from contextlib import ExitStack
+
+import concourse.masks as masks
+import concourse.mybir as mybir
+
+F32 = mybir.dt.float32
+BF16 = mybir.dt.bfloat16
+U32 = mybir.dt.uint32
+U8 = mybir.dt.uint8
+FP8X4 = mybir.dt.float8_e4m3fn_x4
+ACT = mybir.ActivationFunctionType
+ALU = mybir.AluOpType
+
+P = 128
+TOKENS = 512
+HIDDEN = 2048
+LATENT = 1536
+HEADS = 16
+NOPE = 128
+ROPE = 64
+HEAD = NOPE + ROPE
+EPS = 1e-6
+
+K_PASS = 4 * P
+PASSES_A = HIDDEN // K_PASS
+PASSES_B = LATENT // K_PASS
+PAIR = 2 * P
+TOKEN_BLOCKS = TOKENS // P
+BANK = 512
+FOUR_HEADS = 4 * HEAD
+
+RAW_BUFS = 10
+FLOPS = 2 * TOKENS * HIDDEN * LATENT + 2 * TOKENS * LATENT * HEADS * HEAD
+
+
+def tile_deepseekv3attention_pa_kernel(
+    tc, hidden_states, cos, sin, wq_a, sq_a, wq_b, sq_b, q_ln_w, out_0, out_1
+):
+    nc = tc.nc
+    with ExitStack() as ctx:
+        keep = ctx.enter_context(tc.tile_pool(name="keep", bufs=1))
+        raw_pool = ctx.enter_context(tc.tile_pool(name="raw_pool", bufs=RAW_BUFS))
+        grouped_pool = ctx.enter_context(tc.tile_pool(name="grouped_pool", bufs=8))
+        weight_pool = ctx.enter_context(tc.tile_pool(name="weight_pool", bufs=2))
+        h_pool = ctx.enter_context(tc.tile_pool(name="h_pool", bufs=2))
+        out_pool = ctx.enter_context(tc.tile_pool(name="out_pool", bufs=2))
+        bank_pool = ctx.enter_context(tc.psum_pool(name="bank_pool", bufs=6))
+        acc_pool = ctx.enter_context(tc.psum_pool(name="acc_pool", bufs=2))
+        ctx.enter_context(tc.manual_schedule())
+
+        sources = (
+            [hidden_states[PAIR * j : PAIR * (j + 1), :] for j in range(TOKENS // PAIR)]
+            + [wq_a[PAIR * j : PAIR * (j + 1), :] for j in range(LATENT // PAIR)]
+            + [wq_b[PAIR * j : PAIR * (j + 1), :] for j in range(HEADS * HEAD // PAIR)]
+        )
+        first_a = TOKENS // PAIR
+        first_b = first_a + LATENT // PAIR
+        raw_tiles = {}
+
+        def load_pair(j):
+            if j < len(sources):
+                rows = sources[j]
+                raw = raw_pool.tile([P, 2, rows.shape[1]], BF16, name="raw", tag="raw")
+                nc.sync.dma_start(out=raw[:], in_=rows.rearrange("(x p) k -> p x k", p=P))
+                raw_tiles[j] = raw
+
+        for j in range(RAW_BUFS):
+            load_pair(j)
+
+        ident = keep.tile([P, P], F32)
+        masks.make_identity(nc, ident[:])
+        ones = keep.tile([P, P], BF16)
+        nc.vector.memset(ones[:], 1.0)
+        eps = keep.tile([P, 1], F32)
+        nc.vector.memset(eps[:], EPS)
+        warm = keep.tile([P, 1], F32)
+        nc.scalar.activation(out=warm[:], in_=eps[:], func=ACT.Sqrt)
+
+        n_a = sq_a.shape[0] * sq_a.shape[1]
+        n_b = sq_b.shape[0] * sq_b.shape[1]
+        row_zero = keep.tile([P, BANK + LATENT], BF16)
+        nc.vector.memset(row_zero[:], 0.0)
+        nc.scalar.dma_start(out=row_zero[0:1, 0:n_a], in_=sq_a.rearrange("a b -> (a b)").unsqueeze(0))
+        nc.scalar.dma_start(
+            out=row_zero[0:1, n_a : n_a + n_b], in_=sq_b.rearrange("a b -> (a b)").unsqueeze(0)
+        )
+        nc.scalar.dma_start(out=row_zero[0:1, BANK : BANK + LATENT], in_=q_ln_w.unsqueeze(0))
+        cos_sb = keep.tile([P, TOKEN_BLOCKS, ROPE], BF16)
+        nc.scalar.dma_start(out=cos_sb[:], in_=cos.rearrange("(b p) j -> p b j", p=P))
+        sin_sb = keep.tile([P, TOKEN_BLOCKS, ROPE], BF16)
+        nc.scalar.dma_start(out=sin_sb[:], in_=sin.rearrange("(b p) j -> p b j", p=P))
+
+        spread = []
+        for n in range(1 + LATENT // BANK):
+            bank = bank_pool.tile([P, 2, PAIR], F32, name="bank", tag="bank")
+            nc.tensor.matmul(
+                out=bank[:].rearrange("p u s -> p (u s)"),
+                lhsT=ones[:],
+                rhs=row_zero[:, BANK * n : BANK * (n + 1)],
+                start=True,
+                stop=True,
+            )
+            spread.append(bank[:].rearrange("p u s -> p (u s)"))
+
+        def factor_table(flat, blocks, passes):
+            factors = keep.tile([P, passes, blocks, 4], BF16, name="factors%d" % passes)
+            by_k = flat.rearrange("p (o g u f) -> p g o u f", g=passes, u=2, f=2)
+            for half in range(2):
+                rows = slice(64 * half, 64 * (half + 1))
+                for g in range(passes):
+                    nc.vector.tensor_copy(
+                        out=factors[rows, g, :, :].rearrange("p o (u e) -> p o u e", e=2),
+                        in_=by_k[rows, g, :, :, half].unsqueeze(3).to_broadcast([64, blocks, 2, 2]),
+                    )
+            return factors
+
+        factors_a = factor_table(spread[0][:, 0:n_a], sq_a.shape[0], PASSES_A)
+        factors_b = factor_table(spread[0][:, n_a : n_a + n_b], sq_b.shape[0], PASSES_B)
+        gain = keep.tile([P, LATENT], F32)
+        for n in range(LATENT // BANK):
+            nc.scalar.copy(out=gain[:, BANK * n : BANK * (n + 1)], in_=spread[1 + n])
+
+        half_rope = ROPE // 2
+        sin_swapped = keep.tile([P, TOKEN_BLOCKS, ROPE], BF16)
+        nc.vector.tensor_copy(out=sin_swapped[:, :, 0:half_rope], in_=sin_sb[:, :, half_rope:ROPE])
+        nc.vector.tensor_scalar(
+            out=sin_swapped[:, :, half_rope:ROPE],
+            in0=sin_sb[:, :, 0:half_rope],
+            scalar1=-1.0,
+            scalar2=None,
+            op0=ALU.mult,
+        )
+
+        def transpose_pair(pair_tile, passes):
+            banks = []
+            for g in range(passes):
+                bank = bank_pool.tile([P, 2, PAIR], F32, name="bank", tag="bank")
+                for u in range(2):
+                    first = (K_PASS // 2) * g + P * u
+                    for x in range(2):
+                        nc.tensor.transpose(
+                            bank[:, u, P * x : P * (x + 1)],
+                            pair_tile[:, x, :].bitcast(F32)[:, first : first + P],
+                            ident[:],
+                        )
+                banks.append(bank)
+            return banks
+
+        def copy_out(bank):
+            grouped = grouped_pool.tile([P, PAIR, 4], BF16, name="grouped", tag="grouped", align_bytes=64)
+            nc.scalar.copy(out=grouped[:].bitcast(F32), in_=bank[:].rearrange("p u r -> p r u"))
+            return grouped
+
+        def scale_out(bank, factors):
+            grouped = grouped_pool.tile([P, PAIR, 4], BF16, name="grouped", tag="grouped", align_bytes=64)
+            nc.vector.tensor_tensor(
+                out=grouped[:].rearrange("p (x r) (u e) -> p x r u e", x=2, e=2),
+                in0=bank[:].bitcast(BF16).rearrange("p u (x r e) -> p x r u e", x=2, e=2),
+                in1=factors.rearrange("p x (u e) -> p x u e", e=2)
+                .unsqueeze(2)
+                .to_broadcast([P, 2, P, 2, 2]),
+                op=ALU.mult,
+            )
+            return grouped
+
+        def quantise(grouped, codes, scales):
+            nc.vector.quantize_mx(
+                out=codes.bitcast(FP8X4), scales=scales, in_=grouped[:].rearrange("p r t -> p (r t)")
+            )
+
+        def quantise_weights(first_pair, n_pairs, passes, factors, first_block):
+            codes = weight_pool.tile(
+                [P, passes, PAIR * n_pairs], U32, name="w_codes", tag="w_codes", align_bytes=64
+            )
+            scales = weight_pool.tile(
+                [P, passes, PAIR * n_pairs], U8, name="w_scales", tag="w_scales", align_bytes=64
+            )
+            staged = []
+            for j in range(n_pairs):
+                banks = transpose_pair(raw_tiles[first_pair + j], passes)
+                load_pair(first_pair + j + RAW_BUFS)
+                block = first_block + 2 * j
+                for g in range(passes):
+                    staged.append((scale_out(banks[g], factors[:, g, block : block + 2, :]), g, j))
+            for grouped, g, j in staged:
+                cols = slice(PAIR * j, PAIR * (j + 1))
+                quantise(grouped, codes[:, g, cols], scales[:, g, cols])
+            return codes, scales
+
+        def stage_activations(pair_tile, passes):
+            return [copy_out(bank) for bank in transpose_pair(pair_tile, passes)]
+
+        def quantise_activations(staged, j, codes, scales):
+            cols = slice(PAIR * j, PAIR * (j + 1))
+            for g in range(len(staged)):
+                quantise(staged[g], codes[:, g, cols], scales[:, g, cols])
+
+        def multiply(acc, act_codes, act_scales, b, w_codes, w_scales, passes):
+            tokens = slice(P * b, P * (b + 1))
+            for g in range(passes):
+                nc.tensor.matmul_mx(
+                    out=acc,
+                    lhsT=act_codes[:, g, tokens].bitcast(FP8X4),
+                    lhsT_scale=act_scales[:, g, tokens],
+                    rhs=w_codes[:, g, :].bitcast(FP8X4),
+                    rhs_scale=w_scales[:, g, :],
+                    start=(g == 0),
+                    stop=(g == passes - 1),
+                )
+
+        x_codes = keep.tile([P, PASSES_A, TOKENS], U32, align_bytes=64)
+        x_scales = keep.tile([P, PASSES_A, TOKENS], U8, align_bytes=64)
+        for j in range(TOKENS // PAIR):
+            quantise_activations(stage_activations(raw_tiles[j], PASSES_A), j, x_codes, x_scales)
+            load_pair(j + RAW_BUFS)
+
+        latent = keep.tile([P, TOKEN_BLOCKS, LATENT], F32)
+        n_groups_a = LATENT // BANK
+        sum_sq = keep.tile([P, TOKEN_BLOCKS, n_groups_a], F32)
+        h_codes = keep.tile([P, PASSES_B, TOKENS], U32, align_bytes=64)
+        h_scales = keep.tile([P, PASSES_B, TOKENS], U8, align_bytes=64)
+
+        def latent_columns(c, w_codes, w_scales):
+            for b in range(TOKEN_BLOCKS):
+                acc = acc_pool.tile([P, BANK], F32, name="acc", tag="acc")
+                multiply(acc[:], x_codes, x_scales, b, w_codes, w_scales, PASSES_A)
+                squares = out_pool.tile([P, BANK], BF16, name="squares", tag="squares")
+                nc.scalar.activation(
+                    out=squares[:], in_=acc[:], func=ACT.Square, accum_out=sum_sq[:, b, c : c + 1]
+                )
+                nc.scalar.copy(out=latent[:, b, BANK * c : BANK * (c + 1)], in_=acc[:])
+
+        def normalise():
+            unused = keep.tile([P, TOKEN_BLOCKS, n_groups_a], F32)
+            total = keep.tile([P, TOKEN_BLOCKS], F32)
+            rms = keep.tile([P, TOKEN_BLOCKS], F32)
+            inv_rms = keep.tile([P, TOKEN_BLOCKS], F32)
+            staged = []
+            for j in range(TOKENS // PAIR):
+                h_pair = h_pool.tile([P, 2, LATENT], BF16, name="h_pair", tag="h_pair")
+                for x in range(2):
+                    b = 2 * j + x
+                    one = slice(b, b + 1)
+                    nc.scalar.activation(
+                        out=unused[:, b, :], in_=sum_sq[:, b, :], func=ACT.Copy, accum_out=total[:, one]
+                    )
+                    nc.scalar.activation(
+                        out=rms[:, one], in_=total[:, one], func=ACT.Sqrt, scale=1.0 / LATENT, bias=eps[:]
+                    )
+                    nc.vector.reciprocal(out=inv_rms[:, one], in_=rms[:, one])
+                    nc.vector.scalar_tensor_tensor(
+                        out=h_pair[:, x, :],
+                        in0=latent[:, b, :],
+                        scalar=inv_rms[:, one],
+                        in1=gain[:],
+                        op0=ALU.mult,
+                        op1=ALU.mult,
+                    )
+                staged.append(stage_activations(h_pair, PASSES_B))
+            for j in range(TOKENS // PAIR):
+                quantise_activations(staged[j], j, h_codes, h_scales)
+
+        nope_out = out_0.rearrange("(b p) h x -> p b (h x)", p=P)
+        rope_out = out_1.rearrange("(b p) h j -> p b (h j)", p=P)
+
+        def query_columns(m, second, w_codes, w_scales):
+            width = PAIR if second else BANK
+            n_nope = 1 if second else 3
+            nope_sb = out_pool.tile([P, TOKEN_BLOCKS, n_nope, NOPE], F32, name="nope_sb", tag="nope_sb")
+            rope_sb = out_pool.tile([P, TOKEN_BLOCKS, 2, ROPE], F32, name="rope_sb", tag="rope_sb")
+            for b in range(TOKEN_BLOCKS):
+                acc = acc_pool.tile([P, BANK], F32, name="acc", tag="acc")
+                multiply(acc[:, 0:width], h_codes, h_scales, b, w_codes, w_scales, PASSES_B)
+                by_head = acc[:, 0 : 2 * HEAD].rearrange("p (h x) -> p h x", x=HEAD)
+                if second:
+                    nc.scalar.copy(out=rope_sb[:, b, :, :], in_=by_head[:, :, 0:ROPE])
+                    nc.scalar.copy(out=nope_sb[:, b, 0, :], in_=acc[:, ROPE:HEAD])
+                else:
+                    nc.scalar.copy(out=nope_sb[:, b, 0:2, :], in_=by_head[:, :, 0:NOPE])
+                    nc.scalar.copy(out=nope_sb[:, b, 2, :], in_=acc[:, 2 * HEAD : BANK])
+                    nc.scalar.copy(out=rope_sb[:, b, :, :], in_=by_head[:, :, NOPE:HEAD])
+            first_nope = NOPE * (4 * m + 3 * second)
+            nc.sync.dma_start(
+                out=nope_out[:, :, first_nope : first_nope + NOPE * n_nope],
+                in_=nope_sb[:].rearrange("p b h x -> p b (h x)"),
+            )
+            return rope_sb
+
+        def rotate(m, second, rope_sb):
+            shape = [P, TOKEN_BLOCKS, 2, ROPE]
+            straight = out_pool.tile(shape, F32, name="straight", tag="straight")
+            nc.vector.tensor_tensor(
+                out=straight[:], in0=rope_sb[:], in1=cos_sb[:].unsqueeze(2).to_broadcast(shape), op=ALU.mult
+            )
+            crossed = out_pool.tile(shape, F32, name="crossed", tag="crossed")
+            nc.vector.tensor_tensor(
+                out=crossed[:], in0=rope_sb[:], in1=sin_swapped[:].unsqueeze(2).to_broadcast(shape), op=ALU.mult
+            )
+            rotated = out_pool.tile(shape, F32, name="rotated", tag="rotated")
+            low = slice(0, half_rope)
+            high = slice(half_rope, ROPE)
+            nc.vector.tensor_tensor(
+                out=rotated[:, :, :, low], in0=straight[:, :, :, low], in1=crossed[:, :, :, high], op=ALU.add
+            )
+            nc.vector.tensor_tensor(
+                out=rotated[:, :, :, high], in0=straight[:, :, :, high], in1=crossed[:, :, :, low], op=ALU.add
+            )
+            first_rope = ROPE * (4 * m + 2 * second)
+            nc.sync.dma_start(
+                out=rope_out[:, :, first_rope : first_rope + 2 * ROPE],
+                in_=rotated[:].rearrange("p b h j -> p b (h j)"),
+            )
+
+        groups = [(first_a + 2 * c, 2, PASSES_A, factors_a, 4 * c) for c in range(n_groups_a)]
+        for m in range(HEADS // 4):
+            groups.append((first_b + 3 * m, 2, PASSES_B, factors_b, 6 * m))
+            groups.append((first_b + 3 * m + 2, 1, PASSES_B, factors_b, 6 * m + 4))
+
+        ready = quantise_weights(*groups[0])
+        for i in range(len(groups)):
+            following = quantise_weights(*groups[i + 1]) if i + 1 < len(groups) else None
+            if i < n_groups_a:
+                latent_columns(i, *ready)
+                if i == n_groups_a - 1:
+                    normalise()
+            else:
+                m, second = divmod(i - n_groups_a, 2)
+                rotate(m, second, query_columns(m, second, *ready))
+            ready = following

@@ -44,17 +44,30 @@ def tile_deepseekv3attention_pa_kernel(
         weight_pool = ctx.enter_context(tc.tile_pool(name="weight_pool", bufs=2))
         h_pool = ctx.enter_context(tc.tile_pool(name="h_pool", bufs=2))
         out_pool = ctx.enter_context(tc.tile_pool(name="out_pool", bufs=2))
-        bank_pool = ctx.enter_context(tc.psum_pool(name="bank_pool", bufs=6))
-        acc_pool = ctx.enter_context(tc.psum_pool(name="acc_pool", bufs=2))
+        bank_pool = ctx.enter_context(tc.psum_pool(name="bank_pool", bufs=5))
+        acc_pool = ctx.enter_context(tc.psum_pool(name="acc_pool", bufs=3))
         ctx.enter_context(tc.manual_schedule())
 
-        sources = (
-            [hidden_states[PAIR * j : PAIR * (j + 1), :] for j in range(TOKENS // PAIR)]
-            + [wq_a[PAIR * j : PAIR * (j + 1), :] for j in range(LATENT // PAIR)]
-            + [wq_b[PAIR * j : PAIR * (j + 1), :] for j in range(HEADS * HEAD // PAIR)]
+        n_a = sq_a.shape[0] * sq_a.shape[1]
+        n_b = sq_b.shape[0] * sq_b.shape[1]
+        row_zero = keep.tile([P, BANK + LATENT], BF16)
+        nc.vector.memset(row_zero[:], 0.0)
+        nc.scalar.dma_start(out=row_zero[0:1, 0:n_a], in_=sq_a.rearrange("a b -> (a b)").unsqueeze(0))
+        nc.scalar.dma_start(
+            out=row_zero[0:1, n_a : n_a + n_b], in_=sq_b.rearrange("a b -> (a b)").unsqueeze(0)
         )
-        first_a = TOKENS // PAIR
-        first_b = first_a + LATENT // PAIR
+        nc.scalar.dma_start(out=row_zero[0:1, BANK : BANK + LATENT], in_=q_ln_w.unsqueeze(0))
+        cos_bf = keep.tile([P, TOKEN_BLOCKS, ROPE], BF16)
+        nc.scalar.dma_start(out=cos_bf[:], in_=cos.rearrange("(b p) j -> p b j", p=P))
+        sin_bf = keep.tile([P, TOKEN_BLOCKS, ROPE], BF16)
+        nc.scalar.dma_start(out=sin_bf[:], in_=sin.rearrange("(b p) j -> p b j", p=P))
+
+        pairs_x = [hidden_states[PAIR * j : PAIR * (j + 1), :] for j in range(TOKENS // PAIR)]
+        pairs_a = [wq_a[PAIR * j : PAIR * (j + 1), :] for j in range(LATENT // PAIR)]
+        pairs_b = [wq_b[PAIR * j : PAIR * (j + 1), :] for j in range(HEADS * HEAD // PAIR)]
+        sources = pairs_a[0:2] + pairs_x + pairs_a[2:] + pairs_b
+        first_x = 2
+        first_b = len(pairs_x) + len(pairs_a)
         raw_tiles = {}
 
         def load_pair(j):
@@ -75,20 +88,6 @@ def tile_deepseekv3attention_pa_kernel(
         nc.vector.memset(eps[:], EPS)
         warm = keep.tile([P, 1], F32)
         nc.scalar.activation(out=warm[:], in_=eps[:], func=ACT.Sqrt)
-
-        n_a = sq_a.shape[0] * sq_a.shape[1]
-        n_b = sq_b.shape[0] * sq_b.shape[1]
-        row_zero = keep.tile([P, BANK + LATENT], BF16)
-        nc.vector.memset(row_zero[:], 0.0)
-        nc.scalar.dma_start(out=row_zero[0:1, 0:n_a], in_=sq_a.rearrange("a b -> (a b)").unsqueeze(0))
-        nc.scalar.dma_start(
-            out=row_zero[0:1, n_a : n_a + n_b], in_=sq_b.rearrange("a b -> (a b)").unsqueeze(0)
-        )
-        nc.scalar.dma_start(out=row_zero[0:1, BANK : BANK + LATENT], in_=q_ln_w.unsqueeze(0))
-        cos_sb = keep.tile([P, TOKEN_BLOCKS, ROPE], BF16)
-        nc.scalar.dma_start(out=cos_sb[:], in_=cos.rearrange("(b p) j -> p b j", p=P))
-        sin_sb = keep.tile([P, TOKEN_BLOCKS, ROPE], BF16)
-        nc.scalar.dma_start(out=sin_sb[:], in_=sin.rearrange("(b p) j -> p b j", p=P))
 
         spread = []
         for n in range(1 + LATENT // BANK):
@@ -121,20 +120,20 @@ def tile_deepseekv3attention_pa_kernel(
             nc.scalar.copy(out=gain[:, BANK * n : BANK * (n + 1)], in_=spread[1 + n])
 
         half_rope = ROPE // 2
-        sin_swapped = keep.tile([P, TOKEN_BLOCKS, ROPE], BF16)
-        nc.vector.tensor_copy(out=sin_swapped[:, :, 0:half_rope], in_=sin_sb[:, :, half_rope:ROPE])
-        nc.vector.tensor_scalar(
-            out=sin_swapped[:, :, half_rope:ROPE],
-            in0=sin_sb[:, :, 0:half_rope],
-            scalar1=-1.0,
-            scalar2=None,
-            op0=ALU.mult,
+        low = slice(0, half_rope)
+        high = slice(half_rope, ROPE)
+        cos_sb = keep.tile([P, TOKEN_BLOCKS, ROPE], F32)
+        nc.gpsimd.tensor_copy(out=cos_sb[:], in_=cos_bf[:])
+        sin_swapped = keep.tile([P, TOKEN_BLOCKS, ROPE], F32)
+        nc.gpsimd.tensor_copy(out=sin_swapped[:, :, low], in_=sin_bf[:, :, high])
+        nc.gpsimd.tensor_scalar(
+            out=sin_swapped[:, :, high], in0=sin_bf[:, :, low], scalar1=-1.0, scalar2=0.0, op0=ALU.mult, op1=ALU.add
         )
 
-        def transpose_pair(pair_tile, passes):
+        def transpose_pair(pair_tile, passes, pool, tag):
             banks = []
             for g in range(passes):
-                bank = bank_pool.tile([P, 2, PAIR], F32, name="bank", tag="bank")
+                bank = pool.tile([P, 2, PAIR], F32, name=tag, tag=tag)
                 for u in range(2):
                     first = (K_PASS // 2) * g + P * u
                     for x in range(2):
@@ -177,7 +176,7 @@ def tile_deepseekv3attention_pa_kernel(
             )
             staged = []
             for j in range(n_pairs):
-                banks = transpose_pair(raw_tiles[first_pair + j], passes)
+                banks = transpose_pair(raw_tiles[first_pair + j], passes, bank_pool, "bank")
                 load_pair(first_pair + j + RAW_BUFS)
                 block = first_block + 2 * j
                 for g in range(passes):
@@ -186,9 +185,6 @@ def tile_deepseekv3attention_pa_kernel(
                 cols = slice(PAIR * j, PAIR * (j + 1))
                 quantise(grouped, codes[:, g, cols], scales[:, g, cols])
             return codes, scales
-
-        def stage_activations(pair_tile, passes):
-            return [copy_out(bank) for bank in transpose_pair(pair_tile, passes)]
 
         def quantise_activations(staged, j, codes, scales):
             cols = slice(PAIR * j, PAIR * (j + 1))
@@ -210,15 +206,21 @@ def tile_deepseekv3attention_pa_kernel(
 
         x_codes = keep.tile([P, PASSES_A, TOKENS], U32, align_bytes=64)
         x_scales = keep.tile([P, PASSES_A, TOKENS], U8, align_bytes=64)
-        for j in range(TOKENS // PAIR):
-            quantise_activations(stage_activations(raw_tiles[j], PASSES_A), j, x_codes, x_scales)
-            load_pair(j + RAW_BUFS)
-
         latent = keep.tile([P, TOKEN_BLOCKS, LATENT], F32)
         n_groups_a = LATENT // BANK
         sum_sq = keep.tile([P, TOKEN_BLOCKS, n_groups_a], F32)
+        unused = keep.tile([P, TOKEN_BLOCKS, n_groups_a], F32)
+        total = keep.tile([P, TOKEN_BLOCKS], F32)
+        rms = keep.tile([P, TOKEN_BLOCKS], F32)
+        inv_rms = keep.tile([P, TOKEN_BLOCKS], F32)
         h_codes = keep.tile([P, PASSES_B, TOKENS], U32, align_bytes=64)
         h_scales = keep.tile([P, PASSES_B, TOKENS], U8, align_bytes=64)
+
+        def quantise_hidden_states():
+            for j in range(TOKENS // PAIR):
+                banks = transpose_pair(raw_tiles[first_x + j], PASSES_A, bank_pool, "bank")
+                load_pair(first_x + j + RAW_BUFS)
+                quantise_activations([copy_out(bank) for bank in banks], j, x_codes, x_scales)
 
         def latent_columns(c, w_codes, w_scales):
             for b in range(TOKEN_BLOCKS):
@@ -229,17 +231,7 @@ def tile_deepseekv3attention_pa_kernel(
                     out=squares[:], in_=acc[:], func=ACT.Square, accum_out=sum_sq[:, b, c : c + 1]
                 )
                 nc.scalar.copy(out=latent[:, b, BANK * c : BANK * (c + 1)], in_=acc[:])
-
-        def normalise():
-            unused = keep.tile([P, TOKEN_BLOCKS, n_groups_a], F32)
-            total = keep.tile([P, TOKEN_BLOCKS], F32)
-            rms = keep.tile([P, TOKEN_BLOCKS], F32)
-            inv_rms = keep.tile([P, TOKEN_BLOCKS], F32)
-            staged = []
-            for j in range(TOKENS // PAIR):
-                h_pair = h_pool.tile([P, 2, LATENT], BF16, name="h_pair", tag="h_pair")
-                for x in range(2):
-                    b = 2 * j + x
+                if c == n_groups_a - 1:
                     one = slice(b, b + 1)
                     nc.scalar.activation(
                         out=unused[:, b, :], in_=sum_sq[:, b, :], func=ACT.Copy, accum_out=total[:, one]
@@ -247,6 +239,14 @@ def tile_deepseekv3attention_pa_kernel(
                     nc.scalar.activation(
                         out=rms[:, one], in_=total[:, one], func=ACT.Sqrt, scale=1.0 / LATENT, bias=eps[:]
                     )
+
+        def normalise():
+            staged = []
+            for j in range(TOKENS // PAIR):
+                h_pair = h_pool.tile([P, 2, LATENT], BF16, name="h_pair", tag="h_pair")
+                for x in range(2):
+                    b = 2 * j + x
+                    one = slice(b, b + 1)
                     nc.vector.reciprocal(out=inv_rms[:, one], in_=rms[:, one])
                     nc.vector.scalar_tensor_tensor(
                         out=h_pair[:, x, :],
@@ -256,7 +256,7 @@ def tile_deepseekv3attention_pa_kernel(
                         op0=ALU.mult,
                         op1=ALU.mult,
                     )
-                staged.append(stage_activations(h_pair, PASSES_B))
+                staged.append([copy_out(bank) for bank in transpose_pair(h_pair, PASSES_B, acc_pool, "acc")])
             for j in range(TOKENS // PAIR):
                 quantise_activations(staged[j], j, h_codes, h_scales)
 
@@ -276,9 +276,9 @@ def tile_deepseekv3attention_pa_kernel(
                     nc.scalar.copy(out=rope_sb[:, b, :, :], in_=by_head[:, :, 0:ROPE])
                     nc.scalar.copy(out=nope_sb[:, b, 0, :], in_=acc[:, ROPE:HEAD])
                 else:
+                    nc.scalar.copy(out=rope_sb[:, b, :, :], in_=by_head[:, :, NOPE:HEAD])
                     nc.scalar.copy(out=nope_sb[:, b, 0:2, :], in_=by_head[:, :, 0:NOPE])
                     nc.scalar.copy(out=nope_sb[:, b, 2, :], in_=acc[:, 2 * HEAD : BANK])
-                    nc.scalar.copy(out=rope_sb[:, b, :, :], in_=by_head[:, :, NOPE:HEAD])
             first_nope = NOPE * (4 * m + 3 * second)
             nc.sync.dma_start(
                 out=nope_out[:, :, first_nope : first_nope + NOPE * n_nope],
@@ -286,23 +286,21 @@ def tile_deepseekv3attention_pa_kernel(
             )
             return rope_sb
 
-        def rotate(m, second, rope_sb):
+        def rotate(m, second, rope_sb, engine):
             shape = [P, TOKEN_BLOCKS, 2, ROPE]
             straight = out_pool.tile(shape, F32, name="straight", tag="straight")
-            nc.vector.tensor_tensor(
+            engine.tensor_tensor(
                 out=straight[:], in0=rope_sb[:], in1=cos_sb[:].unsqueeze(2).to_broadcast(shape), op=ALU.mult
             )
             crossed = out_pool.tile(shape, F32, name="crossed", tag="crossed")
-            nc.vector.tensor_tensor(
+            engine.tensor_tensor(
                 out=crossed[:], in0=rope_sb[:], in1=sin_swapped[:].unsqueeze(2).to_broadcast(shape), op=ALU.mult
             )
             rotated = out_pool.tile(shape, F32, name="rotated", tag="rotated")
-            low = slice(0, half_rope)
-            high = slice(half_rope, ROPE)
-            nc.vector.tensor_tensor(
+            engine.tensor_tensor(
                 out=rotated[:, :, :, low], in0=straight[:, :, :, low], in1=crossed[:, :, :, high], op=ALU.add
             )
-            nc.vector.tensor_tensor(
+            engine.tensor_tensor(
                 out=rotated[:, :, :, high], in0=straight[:, :, :, high], in1=crossed[:, :, :, low], op=ALU.add
             )
             first_rope = ROPE * (4 * m + 2 * second)
@@ -311,12 +309,15 @@ def tile_deepseekv3attention_pa_kernel(
                 in_=rotated[:].rearrange("p b h j -> p b (h j)"),
             )
 
-        groups = [(first_a + 2 * c, 2, PASSES_A, factors_a, 4 * c) for c in range(n_groups_a)]
+        groups = [
+            (2 * c + (len(pairs_x) if c > 0 else 0), 2, PASSES_A, factors_a, 4 * c) for c in range(n_groups_a)
+        ]
         for m in range(HEADS // 4):
             groups.append((first_b + 3 * m, 2, PASSES_B, factors_b, 6 * m))
             groups.append((first_b + 3 * m + 2, 1, PASSES_B, factors_b, 6 * m + 4))
 
         ready = quantise_weights(*groups[0])
+        quantise_hidden_states()
         for i in range(len(groups)):
             following = quantise_weights(*groups[i + 1]) if i + 1 < len(groups) else None
             if i < n_groups_a:
@@ -325,5 +326,6 @@ def tile_deepseekv3attention_pa_kernel(
                     normalise()
             else:
                 m, second = divmod(i - n_groups_a, 2)
-                rotate(m, second, query_columns(m, second, *ready))
+                engine = nc.gpsimd if i + 2 < len(groups) else nc.vector
+                rotate(m, second, query_columns(m, second, *ready), engine)
             ready = following

@@ -326,6 +326,5 @@ def tile_deepseekv3attention_pa_kernel(
                     normalise()
             else:
                 m, second = divmod(i - n_groups_a, 2)
-                engine = nc.gpsimd if i + 2 < len(groups) else nc.vector
-                rotate(m, second, query_columns(m, second, *ready), engine)
+                rotate(m, second, query_columns(m, second, *ready), nc.vector)
             ready = following

@@ -29,7 +29,9 @@ TOKEN_BLOCKS = TOKENS // P
 BANK = 512
 FOUR_HEADS = 4 * HEAD
 
-RAW_BUFS = 10
+WOVEN_B = PASSES_B - 1
+LAG = 2
+RAW_BUFS = 8
 FLOPS = 2 * TOKENS * HIDDEN * LATENT + 2 * TOKENS * LATENT * HEADS * HEAD
 
 
@@ -41,9 +43,9 @@ def tile_deepseekv3attention_pa_kernel(
         keep = ctx.enter_context(tc.tile_pool(name="keep", bufs=1))
         raw_pool = ctx.enter_context(tc.tile_pool(name="raw_pool", bufs=RAW_BUFS))
         grouped_pool = ctx.enter_context(tc.tile_pool(name="grouped_pool", bufs=8))
-        weight_pool = ctx.enter_context(tc.tile_pool(name="weight_pool", bufs=2))
+        weight_pool = ctx.enter_context(tc.tile_pool(name="weight_pool", bufs=3))
         h_pool = ctx.enter_context(tc.tile_pool(name="h_pool", bufs=2))
-        out_pool = ctx.enter_context(tc.tile_pool(name="out_pool", bufs=2))
+        out_pool = ctx.enter_context(tc.tile_pool(name="out_pool", bufs=3))
         bank_pool = ctx.enter_context(tc.psum_pool(name="bank_pool", bufs=5))
         acc_pool = ctx.enter_context(tc.psum_pool(name="acc_pool", bufs=3))
         ctx.enter_context(tc.manual_schedule())
@@ -52,15 +54,15 @@ def tile_deepseekv3attention_pa_kernel(
         n_b = sq_b.shape[0] * sq_b.shape[1]
         row_zero = keep.tile([P, BANK + LATENT], BF16)
         nc.vector.memset(row_zero[:], 0.0)
-        nc.scalar.dma_start(out=row_zero[0:1, 0:n_a], in_=sq_a.rearrange("a b -> (a b)").unsqueeze(0))
-        nc.scalar.dma_start(
+        nc.sync.dma_start(out=row_zero[0:1, 0:n_a], in_=sq_a.rearrange("a b -> (a b)").unsqueeze(0))
+        nc.sync.dma_start(
             out=row_zero[0:1, n_a : n_a + n_b], in_=sq_b.rearrange("a b -> (a b)").unsqueeze(0)
         )
-        nc.scalar.dma_start(out=row_zero[0:1, BANK : BANK + LATENT], in_=q_ln_w.unsqueeze(0))
+        nc.sync.dma_start(out=row_zero[0:1, BANK : BANK + LATENT], in_=q_ln_w.unsqueeze(0))
         cos_bf = keep.tile([P, TOKEN_BLOCKS, ROPE], BF16)
-        nc.scalar.dma_start(out=cos_bf[:], in_=cos.rearrange("(b p) j -> p b j", p=P))
+        nc.sync.dma_start(out=cos_bf[:], in_=cos.rearrange("(b p) j -> p b j", p=P))
         sin_bf = keep.tile([P, TOKEN_BLOCKS, ROPE], BF16)
-        nc.scalar.dma_start(out=sin_bf[:], in_=sin.rearrange("(b p) j -> p b j", p=P))
+        nc.sync.dma_start(out=sin_bf[:], in_=sin.rearrange("(b p) j -> p b j", p=P))
 
         pairs_x = [hidden_states[PAIR * j : PAIR * (j + 1), :] for j in range(TOKENS // PAIR)]
         pairs_a = [wq_a[PAIR * j : PAIR * (j + 1), :] for j in range(LATENT // PAIR)]
@@ -115,6 +117,15 @@ def tile_deepseekv3attention_pa_kernel(
 
         factors_a = factor_table(spread[0][:, 0:n_a], sq_a.shape[0], PASSES_A)
         factors_b = factor_table(spread[0][:, n_a : n_a + n_b], sq_b.shape[0], PASSES_B)
+        factors_woven = keep.tile([P, sq_b.shape[0]], F32)
+        for quarter in range(4):
+            rows = slice(32 * quarter, 32 * (quarter + 1))
+            nc.vector.tensor_copy(
+                out=factors_woven[rows, :],
+                in_=spread[0][rows, n_a : n_a + n_b].rearrange("p (o k) -> p o k", o=sq_b.shape[0])[
+                    :, :, 4 * WOVEN_B + quarter
+                ],
+            )
         gain = keep.tile([P, LATENT], F32)
         for n in range(LATENT // BANK):
             nc.scalar.copy(out=gain[:, BANK * n : BANK * (n + 1)], in_=spread[1 + n])
@@ -130,18 +141,18 @@ def tile_deepseekv3attention_pa_kernel(
             out=sin_swapped[:, :, high], in0=sin_bf[:, :, low], scalar1=-1.0, scalar2=0.0, op0=ALU.mult, op1=ALU.add
         )
 
-        def transpose_pair(pair_tile, passes, pool, tag):
+        def transpose_pair(pair_tile, passes, pool, tag, woven_pass):
             banks = []
             for g in range(passes):
                 bank = pool.tile([P, 2, PAIR], F32, name=tag, tag=tag)
                 for u in range(2):
-                    first = (K_PASS // 2) * g + P * u
                     for x in range(2):
-                        nc.tensor.transpose(
-                            bank[:, u, P * x : P * (x + 1)],
-                            pair_tile[:, x, :].bitcast(F32)[:, first : first + P],
-                            ident[:],
-                        )
+                        words = pair_tile[:, x, :].bitcast(F32)[:, 2 * P * g : 2 * P * (g + 1)]
+                        if g == woven_pass:
+                            plane = words.rearrange("r (p u) -> r p u", u=2)[:, :, u]
+                        else:
+                            plane = words[:, P * u : P * (u + 1)]
+                        nc.tensor.transpose(bank[:, u, P * x : P * (x + 1)], plane, ident[:])
                 banks.append(bank)
             return banks
 
@@ -162,29 +173,45 @@ def tile_deepseekv3attention_pa_kernel(
             )
             return grouped
 
+        def scale_out_woven(bank, factors):
+            grouped = grouped_pool.tile([P, PAIR, 4], BF16, name="grouped", tag="grouped", align_bytes=64)
+            for x in range(2):
+                rows = slice(P * x, P * (x + 1))
+                nc.scalar.activation(
+                    out=grouped[:, rows, :].rearrange("p r (u e) -> p r u e", e=2),
+                    in_=bank[:, :, rows].bitcast(BF16).rearrange("p u (r e) -> p r u e", e=2),
+                    func=ACT.Copy,
+                    scale=factors[:, x : x + 1],
+                )
+            return grouped
+
         def quantise(grouped, codes, scales):
             nc.vector.quantize_mx(
                 out=codes.bitcast(FP8X4), scales=scales, in_=grouped[:].rearrange("p r t -> p (r t)")
             )
 
-        def quantise_weights(first_pair, n_pairs, passes, factors, first_block):
+        def weight_tiles(first_pair, n_pairs, passes, factors, first_block, woven_pass):
             codes = weight_pool.tile(
                 [P, passes, PAIR * n_pairs], U32, name="w_codes", tag="w_codes", align_bytes=64
             )
             scales = weight_pool.tile(
                 [P, passes, PAIR * n_pairs], U8, name="w_scales", tag="w_scales", align_bytes=64
             )
-            staged = []
-            for j in range(n_pairs):
-                banks = transpose_pair(raw_tiles[first_pair + j], passes, bank_pool, "bank")
-                load_pair(first_pair + j + RAW_BUFS)
-                block = first_block + 2 * j
-                for g in range(passes):
-                    staged.append((scale_out(banks[g], factors[:, g, block : block + 2, :]), g, j))
-            for grouped, g, j in staged:
-                cols = slice(PAIR * j, PAIR * (j + 1))
-                quantise(grouped, codes[:, g, cols], scales[:, g, cols])
             return codes, scales
+
+        def quantise_weights(j, codes, scales, first_pair, n_pairs, passes, factors, first_block, woven_pass):
+            banks = transpose_pair(raw_tiles[first_pair + j], passes, bank_pool, "bank", woven_pass)
+            load_pair(first_pair + j + RAW_BUFS)
+            block = first_block + 2 * j
+            staged = [
+                scale_out_woven(banks[g], factors_woven[:, block : block + 2])
+                if g == woven_pass
+                else scale_out(banks[g], factors[:, g, block : block + 2, :])
+                for g in range(passes)
+            ]
+            cols = slice(PAIR * j, PAIR * (j + 1))
+            for g in range(passes):
+                quantise(staged[g], codes[:, g, cols], scales[:, g, cols])
 
         def quantise_activations(staged, j, codes, scales):
             cols = slice(PAIR * j, PAIR * (j + 1))
@@ -218,12 +245,12 @@ def tile_deepseekv3attention_pa_kernel(
 
         def quantise_hidden_states():
             for j in range(TOKENS // PAIR):
-                banks = transpose_pair(raw_tiles[first_x + j], PASSES_A, bank_pool, "bank")
+                banks = transpose_pair(raw_tiles[first_x + j], PASSES_A, bank_pool, "bank", None)
                 load_pair(first_x + j + RAW_BUFS)
                 quantise_activations([copy_out(bank) for bank in banks], j, x_codes, x_scales)
 
-        def latent_columns(c, w_codes, w_scales):
-            for b in range(TOKEN_BLOCKS):
+        def latent_columns(c, blocks, w_codes, w_scales):
+            for b in blocks:
                 acc = acc_pool.tile([P, BANK], F32, name="acc", tag="acc")
                 multiply(acc[:], x_codes, x_scales, b, w_codes, w_scales, PASSES_A)
                 squares = out_pool.tile([P, BANK], BF16, name="squares", tag="squares")
@@ -256,19 +283,22 @@ def tile_deepseekv3attention_pa_kernel(
                         op0=ALU.mult,
                         op1=ALU.mult,
                     )
-                staged.append([copy_out(bank) for bank in transpose_pair(h_pair, PASSES_B, acc_pool, "acc")])
+                staged.append([copy_out(bank) for bank in transpose_pair(h_pair, PASSES_B, acc_pool, "acc", WOVEN_B)])
             for j in range(TOKENS // PAIR):
                 quantise_activations(staged[j], j, h_codes, h_scales)
 
         nope_out = out_0.rearrange("(b p) h x -> p b (h x)", p=P)
         rope_out = out_1.rearrange("(b p) h j -> p b (h j)", p=P)
 
-        def query_columns(m, second, w_codes, w_scales):
-            width = PAIR if second else BANK
+        def query_tiles(second):
             n_nope = 1 if second else 3
             nope_sb = out_pool.tile([P, TOKEN_BLOCKS, n_nope, NOPE], F32, name="nope_sb", tag="nope_sb")
             rope_sb = out_pool.tile([P, TOKEN_BLOCKS, 2, ROPE], F32, name="rope_sb", tag="rope_sb")
-            for b in range(TOKEN_BLOCKS):
+            return nope_sb, rope_sb
+
+        def query_columns(second, blocks, nope_sb, rope_sb, w_codes, w_scales):
+            width = PAIR if second else BANK
+            for b in blocks:
                 acc = acc_pool.tile([P, BANK], F32, name="acc", tag="acc")
                 multiply(acc[:, 0:width], h_codes, h_scales, b, w_codes, w_scales, PASSES_B)
                 by_head = acc[:, 0 : 2 * HEAD].rearrange("p (h x) -> p h x", x=HEAD)
@@ -279,12 +309,13 @@ def tile_deepseekv3attention_pa_kernel(
                     nc.scalar.copy(out=rope_sb[:, b, :, :], in_=by_head[:, :, NOPE:HEAD])
                     nc.scalar.copy(out=nope_sb[:, b, 0:2, :], in_=by_head[:, :, 0:NOPE])
                     nc.scalar.copy(out=nope_sb[:, b, 2, :], in_=acc[:, 2 * HEAD : BANK])
+
+        def store_unrotated(m, second, nope_sb):
             first_nope = NOPE * (4 * m + 3 * second)
             nc.sync.dma_start(
-                out=nope_out[:, :, first_nope : first_nope + NOPE * n_nope],
+                out=nope_out[:, :, first_nope : first_nope + NOPE * nope_sb.shape[2]],
                 in_=nope_sb[:].rearrange("p b h x -> p b (h x)"),
             )
-            return rope_sb
 
         def rotate(m, second, rope_sb, engine):
             shape = [P, TOKEN_BLOCKS, 2, ROPE]
@@ -310,21 +341,45 @@ def tile_deepseekv3attention_pa_kernel(
             )
 
         groups = [
-            (2 * c + (len(pairs_x) if c > 0 else 0), 2, PASSES_A, factors_a, 4 * c) for c in range(n_groups_a)
+            (2 * c + (len(pairs_x) if c > 0 else 0), 2, PASSES_A, factors_a, 4 * c, None) for c in range(n_groups_a)
         ]
         for m in range(HEADS // 4):
-            groups.append((first_b + 3 * m, 2, PASSES_B, factors_b, 6 * m))
-            groups.append((first_b + 3 * m + 2, 1, PASSES_B, factors_b, 6 * m + 4))
+            groups.append((first_b + 3 * m, 2, PASSES_B, factors_b, 6 * m, WOVEN_B))
+            groups.append((first_b + 3 * m + 2, 1, PASSES_B, factors_b, 6 * m + 4, WOVEN_B))
 
-        ready = quantise_weights(*groups[0])
-        quantise_hidden_states()
+        steps = []
         for i in range(len(groups)):
-            following = quantise_weights(*groups[i + 1]) if i + 1 < len(groups) else None
-            if i < n_groups_a:
-                latent_columns(i, *ready)
-                if i == n_groups_a - 1:
-                    normalise()
-            else:
-                m, second = divmod(i - n_groups_a, 2)
-                rotate(m, second, query_columns(m, second, *ready), nc.vector)
-            ready = following
+            for j in range(groups[i][1]):
+                share = TOKEN_BLOCKS // groups[i][1]
+                steps.append((i, j, range(share * j, share * (j + 1))))
+        weights = {}
+        results = {}
+        waiting = []
+        for s in range(len(steps) + LAG):
+            if s < len(steps):
+                i, j, blocks = steps[s]
+                if j == 0:
+                    weights[i] = weight_tiles(*groups[i])
+                quantise_weights(j, *weights[i], *groups[i])
+            if s == 1:
+                quantise_hidden_states()
+            if len(waiting) > 0 and (waiting[0][0] < s or s >= len(steps)):
+                rotate(*waiting[0][1])
+                waiting = waiting[1:]
+            if s >= LAG:
+                i, j, blocks = steps[s - LAG]
+                last = j == groups[i][1] - 1
+                if i < n_groups_a:
+                    latent_columns(i, blocks, *weights[i])
+                    if last and i == n_groups_a - 1:
+                        normalise()
+                else:
+                    m, second = divmod(i - n_groups_a, 2)
+                    if j == 0:
+                        results[i] = query_tiles(second)
+                    query_columns(second, blocks, *results[i], *weights[i])
+                    if last:
+                        store_unrotated(m, second, results[i][0])
+                        waiting.append((s, (m, second, results[i][1], nc.vector)))
+        for late in waiting:
+            rotate(*late[1])

@@ -21,18 +21,23 @@ ROPE = 64
 HEAD = NOPE + ROPE
 EPS = 1e-6
 
+ROWS = 4
+GROUP = ROWS * P
 K_PASS = 4 * P
 PASSES_A = HIDDEN // K_PASS
 PASSES_B = LATENT // K_PASS
-PAIR = 2 * P
+GROUPS_A = LATENT // GROUP
+GROUPS_B = HEADS * HEAD // GROUP
 TOKEN_BLOCKS = TOKENS // P
-BANK = 512
-FOUR_HEADS = 4 * HEAD
-
-WOVEN_B = PASSES_B - 1
-LAG = 2
-RAW_BUFS = 8
+HALF = HIDDEN // 2
 FLOPS = 2 * TOKENS * HIDDEN * LATENT + 2 * TOKENS * LATENT * HEADS * HEAD
+H_AT = (5, 7)
+RAW_BUFS = {1: 2, 2: 7, 3: 3}
+TOGETHER = 1
+BUDGET_A = 4
+BUDGET_B = 6
+AHEAD = 2
+Q_WIDTH = 640
 
 
 def tile_deepseekv3attention_pa_kernel(
@@ -41,46 +46,58 @@ def tile_deepseekv3attention_pa_kernel(
     nc = tc.nc
     with ExitStack() as ctx:
         keep = ctx.enter_context(tc.tile_pool(name="keep", bufs=1))
-        raw_pool = ctx.enter_context(tc.tile_pool(name="raw_pool", bufs=RAW_BUFS))
-        grouped_pool = ctx.enter_context(tc.tile_pool(name="grouped_pool", bufs=8))
-        weight_pool = ctx.enter_context(tc.tile_pool(name="weight_pool", bufs=3))
-        h_pool = ctx.enter_context(tc.tile_pool(name="h_pool", bufs=2))
-        out_pool = ctx.enter_context(tc.tile_pool(name="out_pool", bufs=3))
-        bank_pool = ctx.enter_context(tc.psum_pool(name="bank_pool", bufs=5))
-        acc_pool = ctx.enter_context(tc.psum_pool(name="acc_pool", bufs=3))
+        raw_pool = ctx.enter_context(tc.tile_pool(name="raw_pool", bufs=1))
+        grouped_pool = ctx.enter_context(tc.tile_pool(name="grouped_pool", bufs=4))
+        weight_pool = ctx.enter_context(tc.tile_pool(name="weight_pool", bufs=16))
+        h_pool = ctx.enter_context(tc.tile_pool(name="h_pool", bufs=3))
+        q_pool = ctx.enter_context(tc.tile_pool(name="q_pool", bufs=3))
+        rope_pool = ctx.enter_context(tc.tile_pool(name="rope_pool", bufs=1))
+        out_pool = ctx.enter_context(tc.tile_pool(name="out_pool", bufs=2))
+        bank_pool = ctx.enter_context(tc.psum_pool(name="bank_pool", bufs=4))
+        acc_pool = ctx.enter_context(tc.psum_pool(name="acc_pool", bufs=4))
         ctx.enter_context(tc.manual_schedule())
 
         n_a = sq_a.shape[0] * sq_a.shape[1]
         n_b = sq_b.shape[0] * sq_b.shape[1]
-        row_zero = keep.tile([P, BANK + LATENT], BF16)
+        row_zero = grouped_pool.tile([P, GROUP + LATENT], BF16, name="grouped", tag="grouped", align_bytes=64)
         nc.vector.memset(row_zero[:], 0.0)
         nc.sync.dma_start(out=row_zero[0:1, 0:n_a], in_=sq_a.rearrange("a b -> (a b)").unsqueeze(0))
         nc.sync.dma_start(
             out=row_zero[0:1, n_a : n_a + n_b], in_=sq_b.rearrange("a b -> (a b)").unsqueeze(0)
         )
-        nc.sync.dma_start(out=row_zero[0:1, BANK : BANK + LATENT], in_=q_ln_w.unsqueeze(0))
         cos_bf = keep.tile([P, TOKEN_BLOCKS, ROPE], BF16)
-        nc.sync.dma_start(out=cos_bf[:], in_=cos.rearrange("(b p) j -> p b j", p=P))
         sin_bf = keep.tile([P, TOKEN_BLOCKS, ROPE], BF16)
-        nc.sync.dma_start(out=sin_bf[:], in_=sin.rearrange("(b p) j -> p b j", p=P))
 
-        pairs_x = [hidden_states[PAIR * j : PAIR * (j + 1), :] for j in range(TOKENS // PAIR)]
-        pairs_a = [wq_a[PAIR * j : PAIR * (j + 1), :] for j in range(LATENT // PAIR)]
-        pairs_b = [wq_b[PAIR * j : PAIR * (j + 1), :] for j in range(HEADS * HEAD // PAIR)]
-        sources = pairs_a[0:2] + pairs_x + pairs_a[2:] + pairs_b
-        first_x = 2
-        first_b = len(pairs_x) + len(pairs_a)
-        raw_tiles = {}
+        def load_small():
+            nc.sync.dma_start(out=row_zero[0:1, GROUP : GROUP + LATENT], in_=q_ln_w.unsqueeze(0))
+            nc.sync.dma_start(out=cos_bf[:], in_=cos.rearrange("(b p) j -> p b j", p=P))
+            nc.sync.dma_start(out=sin_bf[:], in_=sin.rearrange("(b p) j -> p b j", p=P))
 
-        def load_pair(j):
-            if j < len(sources):
-                rows = sources[j]
-                raw = raw_pool.tile([P, 2, rows.shape[1]], BF16, name="raw", tag="raw")
-                nc.sync.dma_start(out=raw[:], in_=rows.rearrange("(x p) k -> p x k", p=P))
-                raw_tiles[j] = raw
+        rows_x = hidden_states.rearrange("(b p) k -> p b k", p=P)
 
-        for j in range(RAW_BUFS):
-            load_pair(j)
+        def weight_rows(weights, n):
+            return weights[GROUP * n : GROUP * (n + 1), :].rearrange("(p r) k -> p r k", r=ROWS)
+
+        raw = {}
+
+        def load(kind, n, first, count):
+            rows = rows_x if kind == "x" else weight_rows(wq_a if kind == "a" else wq_b, n)
+            tag = "raw_%d" % count
+            tile = raw_pool.tile([P, ROWS, K_PASS * count], BF16, name=tag, tag=tag, bufs=RAW_BUFS[count])
+            nc.sync.dma_start(out=tile[:], in_=rows[:, :, K_PASS * first : K_PASS * (first + count)])
+            for g in range(count):
+                raw[(kind, n, first + g)] = tile[:, :, K_PASS * g : K_PASS * (g + 1)]
+
+        loads = []
+        loads.extend([("a", 0, 0, 1), ("x", 0, 0, 2), ("a", 0, 1, 1), ("a", 0, 2, 2), ("x", 0, 2, 2)])
+        for n in range(1, GROUPS_A):
+            loads.extend([("a", n, g, 2) for g in range(0, PASSES_A, 2)])
+        for n in range(GROUPS_B):
+            loads.append(("b", n, 0, PASSES_B))
+        for i in range(len(loads)):
+            load(*loads[i])
+            if i == 3:
+                load_small()
 
         ident = keep.tile([P, P], F32)
         masks.make_identity(nc, ident[:])
@@ -91,44 +108,29 @@ def tile_deepseekv3attention_pa_kernel(
         warm = keep.tile([P, 1], F32)
         nc.scalar.activation(out=warm[:], in_=eps[:], func=ACT.Sqrt)
 
-        spread = []
-        for n in range(1 + LATENT // BANK):
-            bank = bank_pool.tile([P, 2, PAIR], F32, name="bank", tag="bank")
+        def spread(n):
+            bank = bank_pool.tile([P, GROUP], F32, name="bank", tag="bank")
             nc.tensor.matmul(
-                out=bank[:].rearrange("p u s -> p (u s)"),
-                lhsT=ones[:],
-                rhs=row_zero[:, BANK * n : BANK * (n + 1)],
-                start=True,
-                stop=True,
+                out=bank[:], lhsT=ones[:], rhs=row_zero[:, GROUP * n : GROUP * (n + 1)], start=True, stop=True
             )
-            spread.append(bank[:].rearrange("p u s -> p (u s)"))
+            return bank
 
-        def factor_table(flat, blocks, passes):
-            factors = keep.tile([P, passes, blocks, 4], BF16, name="factors%d" % passes)
-            by_k = flat.rearrange("p (o g u f) -> p g o u f", g=passes, u=2, f=2)
-            for half in range(2):
-                rows = slice(64 * half, 64 * (half + 1))
-                for g in range(passes):
-                    nc.vector.tensor_copy(
-                        out=factors[rows, g, :, :].rearrange("p o (u e) -> p o u e", e=2),
-                        in_=by_k[rows, g, :, :, half].unsqueeze(3).to_broadcast([64, blocks, 2, 2]),
-                    )
-            return factors
-
-        factors_a = factor_table(spread[0][:, 0:n_a], sq_a.shape[0], PASSES_A)
-        factors_b = factor_table(spread[0][:, n_a : n_a + n_b], sq_b.shape[0], PASSES_B)
-        factors_woven = keep.tile([P, sq_b.shape[0]], F32)
-        for quarter in range(4):
-            rows = slice(32 * quarter, 32 * (quarter + 1))
-            nc.vector.tensor_copy(
-                out=factors_woven[rows, :],
-                in_=spread[0][rows, n_a : n_a + n_b].rearrange("p (o k) -> p o k", o=sq_b.shape[0])[
-                    :, :, 4 * WOVEN_B + quarter
-                ],
+        bank = spread(0)
+        factors = {}
+        for kind, first, shape in (("a", 0, sq_a.shape), ("b", n_a, sq_b.shape)):
+            table = keep.tile([P, shape[0] // 4, shape[1]], F32, name="factors_" + kind)
+            by_quarter = bank[:, first : first + shape[0] * shape[1]].rearrange(
+                "p (n q c) -> p n q c", q=4, c=shape[1]
             )
+            for quarter in range(4):
+                rows = slice(32 * quarter, 32 * (quarter + 1))
+                nc.scalar.copy(out=table[rows, :, :], in_=by_quarter[rows, :, quarter, :])
+            factors[kind] = table
         gain = keep.tile([P, LATENT], F32)
-        for n in range(LATENT // BANK):
-            nc.scalar.copy(out=gain[:, BANK * n : BANK * (n + 1)], in_=spread[1 + n])
+
+        def spread_gain():
+            for n in range(LATENT // GROUP):
+                nc.scalar.copy(out=gain[:, GROUP * n : GROUP * (n + 1)], in_=spread(1 + n)[:])
 
         half_rope = ROPE // 2
         low = slice(0, half_rope)
@@ -141,245 +143,276 @@ def tile_deepseekv3attention_pa_kernel(
             out=sin_swapped[:, :, high], in0=sin_bf[:, :, low], scalar1=-1.0, scalar2=0.0, op0=ALU.mult, op1=ALU.add
         )
 
-        def transpose_pair(pair_tile, passes, pool, tag, woven_pass):
-            banks = []
-            for g in range(passes):
-                bank = pool.tile([P, 2, PAIR], F32, name=tag, tag=tag)
+        banks = {}
+        grouped = {}
+        codes = {}
+        scales = {}
+
+        def prescale(item):
+            kind, n, g = item
+            if kind in factors:
+                for c in range(ROWS):
+                    block = raw[item][:, :, P * c : P * (c + 1)]
+                    nc.vector.tensor_scalar_mul(
+                        out=block, in0=block, scalar1=factors[kind][:, n, 4 * g + c : 4 * g + c + 1]
+                    )
+
+        def transpose_rows(rows, n_rows):
+            result = []
+            for pair in range(n_rows // 2):
+                bank = bank_pool.tile([P, 2, 2 * P], F32, name="bank", tag="bank")
                 for u in range(2):
                     for x in range(2):
-                        words = pair_tile[:, x, :].bitcast(F32)[:, 2 * P * g : 2 * P * (g + 1)]
-                        if g == woven_pass:
-                            plane = words.rearrange("r (p u) -> r p u", u=2)[:, :, u]
-                        else:
-                            plane = words[:, P * u : P * (u + 1)]
-                        nc.tensor.transpose(bank[:, u, P * x : P * (x + 1)], plane, ident[:])
-                banks.append(bank)
-            return banks
+                        words = rows[:, 2 * pair + x, :].bitcast(F32)[:, P * u : P * (u + 1)]
+                        nc.tensor.transpose(bank[:, u, P * x : P * (x + 1)], words, ident[:])
+                result.append(bank)
+            return result
 
-        def copy_out(bank):
-            grouped = grouped_pool.tile([P, PAIR, 4], BF16, name="grouped", tag="grouped", align_bytes=64)
-            nc.scalar.copy(out=grouped[:].bitcast(F32), in_=bank[:].rearrange("p u r -> p r u"))
-            return grouped
-
-        def scale_out(bank, factors):
-            grouped = grouped_pool.tile([P, PAIR, 4], BF16, name="grouped", tag="grouped", align_bytes=64)
-            nc.vector.tensor_tensor(
-                out=grouped[:].rearrange("p (x r) (u e) -> p x r u e", x=2, e=2),
-                in0=bank[:].bitcast(BF16).rearrange("p u (x r e) -> p x r u e", x=2, e=2),
-                in1=factors.rearrange("p x (u e) -> p x u e", e=2)
-                .unsqueeze(2)
-                .to_broadcast([P, 2, P, 2, 2]),
-                op=ALU.mult,
-            )
-            return grouped
-
-        def scale_out_woven(bank, factors):
-            grouped = grouped_pool.tile([P, PAIR, 4], BF16, name="grouped", tag="grouped", align_bytes=64)
-            for x in range(2):
-                rows = slice(P * x, P * (x + 1))
-                nc.scalar.activation(
-                    out=grouped[:, rows, :].rearrange("p r (u e) -> p r u e", e=2),
-                    in_=bank[:, :, rows].bitcast(BF16).rearrange("p u (r e) -> p r u e", e=2),
-                    func=ACT.Copy,
-                    scale=factors[:, x : x + 1],
+        def copy_out(some_banks):
+            tile = grouped_pool.tile([P, 2 * P * len(some_banks), 4], BF16, name="grouped", tag="grouped", align_bytes=64)
+            for i in range(len(some_banks)):
+                nc.scalar.copy(
+                    out=tile[:, 2 * P * i : 2 * P * (i + 1), :].bitcast(F32),
+                    in_=some_banks[i][:].rearrange("p u r -> p r u"),
                 )
-            return grouped
+            return tile
 
-        def quantise(grouped, codes, scales):
-            nc.vector.quantize_mx(
-                out=codes.bitcast(FP8X4), scales=scales, in_=grouped[:].rearrange("p r t -> p (r t)")
-            )
+        def quantise(tile, out, out_scales):
+            nc.vector.quantize_mx(out=out.bitcast(FP8X4), scales=out_scales, in_=tile[:].rearrange("p r t -> p (r t)"))
 
-        def weight_tiles(first_pair, n_pairs, passes, factors, first_block, woven_pass):
-            codes = weight_pool.tile(
-                [P, passes, PAIR * n_pairs], U32, name="w_codes", tag="w_codes", align_bytes=64
-            )
-            scales = weight_pool.tile(
-                [P, passes, PAIR * n_pairs], U8, name="w_scales", tag="w_scales", align_bytes=64
-            )
-            return codes, scales
-
-        def quantise_weights(j, codes, scales, first_pair, n_pairs, passes, factors, first_block, woven_pass):
-            banks = transpose_pair(raw_tiles[first_pair + j], passes, bank_pool, "bank", woven_pass)
-            load_pair(first_pair + j + RAW_BUFS)
-            block = first_block + 2 * j
-            staged = [
-                scale_out_woven(banks[g], factors_woven[:, block : block + 2])
-                if g == woven_pass
-                else scale_out(banks[g], factors[:, g, block : block + 2, :])
-                for g in range(passes)
-            ]
-            cols = slice(PAIR * j, PAIR * (j + 1))
-            for g in range(passes):
-                quantise(staged[g], codes[:, g, cols], scales[:, g, cols])
-
-        def quantise_activations(staged, j, codes, scales):
-            cols = slice(PAIR * j, PAIR * (j + 1))
-            for g in range(len(staged)):
-                quantise(staged[g], codes[:, g, cols], scales[:, g, cols])
-
-        def multiply(acc, act_codes, act_scales, b, w_codes, w_scales, passes):
-            tokens = slice(P * b, P * (b + 1))
-            for g in range(passes):
-                nc.tensor.matmul_mx(
-                    out=acc,
-                    lhsT=act_codes[:, g, tokens].bitcast(FP8X4),
-                    lhsT_scale=act_scales[:, g, tokens],
-                    rhs=w_codes[:, g, :].bitcast(FP8X4),
-                    rhs_scale=w_scales[:, g, :],
-                    start=(g == 0),
-                    stop=(g == passes - 1),
-                )
-
-        x_codes = keep.tile([P, PASSES_A, TOKENS], U32, align_bytes=64)
-        x_scales = keep.tile([P, PASSES_A, TOKENS], U8, align_bytes=64)
-        latent = keep.tile([P, TOKEN_BLOCKS, LATENT], F32)
-        n_groups_a = LATENT // BANK
-        sum_sq = keep.tile([P, TOKEN_BLOCKS, n_groups_a], F32)
-        unused = keep.tile([P, TOKEN_BLOCKS, n_groups_a], F32)
-        total = keep.tile([P, TOKEN_BLOCKS], F32)
-        rms = keep.tile([P, TOKEN_BLOCKS], F32)
-        inv_rms = keep.tile([P, TOKEN_BLOCKS], F32)
         h_codes = keep.tile([P, PASSES_B, TOKENS], U32, align_bytes=64)
         h_scales = keep.tile([P, PASSES_B, TOKENS], U8, align_bytes=64)
+        x_codes = keep.tile([P, PASSES_A, TOKENS], U32, align_bytes=64)
+        x_scales = keep.tile([P, PASSES_A, TOKENS], U8, align_bytes=64)
+        latents = {}
+        sum_sq = keep.tile([P, TOKEN_BLOCKS, GROUPS_A], F32)
+        mean_sq = keep.tile([P, TOKEN_BLOCKS, GROUPS_A], F32)
+        inv_rms = keep.tile([P, TOKEN_BLOCKS], F32)
+        h_rows = {}
 
-        def quantise_hidden_states():
-            for j in range(TOKENS // PAIR):
-                banks = transpose_pair(raw_tiles[first_x + j], PASSES_A, bank_pool, "bank", None)
-                load_pair(first_x + j + RAW_BUFS)
-                quantise_activations([copy_out(bank) for bank in banks], j, x_codes, x_scales)
+        def transposes(item):
+            kind, n, g = item
+            if kind == "h":
+                banks[item] = []
+                for g in range(PASSES_B):
+                    bank = bank_pool.tile([P, 2, 2 * P], F32, name="bank", tag="bank")
+                    for u in range(2):
+                        for x in range(2):
+                            words = h_rows[2 * n + x][:].bitcast(F32)[:, 2 * P * g + P * u : 2 * P * g + P * (u + 1)]
+                            nc.tensor.transpose(bank[:, u, P * x : P * (x + 1)], words, ident[:])
+                    banks[item].append(bank)
+            else:
+                banks[item] = transpose_rows(raw[item], ROWS)
 
-        def latent_columns(c, blocks, w_codes, w_scales):
-            for b in blocks:
-                acc = acc_pool.tile([P, BANK], F32, name="acc", tag="acc")
-                multiply(acc[:], x_codes, x_scales, b, w_codes, w_scales, PASSES_A)
-                squares = out_pool.tile([P, BANK], BF16, name="squares", tag="squares")
-                nc.scalar.activation(
-                    out=squares[:], in_=acc[:], func=ACT.Square, accum_out=sum_sq[:, b, c : c + 1]
+        def copies_out(item):
+            if item[0] == "h":
+                grouped[item] = [copy_out([bank]) for bank in banks[item]]
+            else:
+                grouped[item] = [copy_out(banks[item])]
+
+        def quantises(item):
+            kind, n, g = item
+            if kind == "h":
+                cols = slice(2 * P * n, 2 * P * (n + 1))
+                for g in range(PASSES_B):
+                    quantise(grouped[item][g], h_codes[:, g, cols], h_scales[:, g, cols])
+            elif kind == "x":
+                quantise(grouped[item][0], x_codes[:, g, :], x_scales[:, g, :])
+            else:
+                w_codes = weight_pool.tile([P, GROUP], U32, name="w_codes", tag="w_codes", align_bytes=64)
+                w_scales = weight_pool.tile([P, GROUP], U8, name="w_scales", tag="w_scales", align_bytes=64)
+                quantise(grouped[item][0], w_codes[:], w_scales[:])
+                codes[item] = w_codes
+                scales[item] = w_scales
+
+        accs = {}
+
+        def multiply(kind, n, b, g, passes):
+            if g == 0:
+                accs[(kind, n, b)] = acc_pool.tile([P, GROUP], F32, name="acc", tag="acc")
+            act_codes, act_scales = (x_codes, x_scales) if kind == "a" else (h_codes, h_scales)
+            tokens = slice(P * b, P * (b + 1))
+            nc.tensor.matmul_mx(
+                out=accs[(kind, n, b)][:],
+                lhsT=act_codes[:, g, tokens].bitcast(FP8X4),
+                lhsT_scale=act_scales[:, g, tokens],
+                rhs=codes[(kind, n, g)][:].bitcast(FP8X4),
+                rhs_scale=scales[(kind, n, g)][:],
+                start=(g == 0),
+                stop=(g == passes - 1),
+            )
+
+        def natural(columns):
+            return columns.rearrange("t (r p) -> t p r", r=ROWS)
+
+        def finish_latent(c, b):
+            acc = accs[("a", c, b)]
+            squares = rope_pool.tile([P, GROUP], BF16, name="squares", tag="squares")
+            nc.scalar.activation(out=squares[:], in_=acc[:], func=ACT.Square, accum_out=sum_sq[:, b, c : c + 1])
+            cols = slice(GROUP * c, GROUP * (c + 1))
+            if b == 0:
+                latents[c] = q_pool.tile([P, TOKEN_BLOCKS, GROUP], F32, name="q_sb", tag="q_sb")
+            nc.vector.tensor_tensor(
+                out=latents[c][:, b, :].rearrange("t (p r) -> t p r", r=ROWS),
+                in0=natural(acc[:]),
+                in1=gain[:, cols].rearrange("t (p r) -> t p r", r=ROWS),
+                op=ALU.mult,
+            )
+            nc.scalar.activation(
+                out=mean_sq[:, b, c : c + 1],
+                in_=sum_sq[:, b, c : c + 1],
+                func=ACT.Sqrt if c == GROUPS_A - 1 else ACT.Identity,
+                scale=1.0 / LATENT,
+                bias=eps[:] if c == 0 else mean_sq[:, b, c - 1 : c],
+            )
+
+        def normalise(b):
+            one = slice(b, b + 1)
+            nc.vector.reciprocal(out=inv_rms[:, one], in_=mean_sq[:, b, GROUPS_A - 1 : GROUPS_A])
+            h_rows[b] = h_pool.tile([P, LATENT], BF16, name="h_row", tag="h_row")
+            for c in range(GROUPS_A):
+                nc.vector.tensor_scalar_mul(
+                    out=h_rows[b][:, GROUP * c : GROUP * (c + 1)], in0=latents[c][:, b, :], scalar1=inv_rms[:, one]
                 )
-                nc.scalar.copy(out=latent[:, b, BANK * c : BANK * (c + 1)], in_=acc[:])
-                if c == n_groups_a - 1:
-                    one = slice(b, b + 1)
-                    nc.scalar.activation(
-                        out=unused[:, b, :], in_=sum_sq[:, b, :], func=ACT.Copy, accum_out=total[:, one]
-                    )
-                    nc.scalar.activation(
-                        out=rms[:, one], in_=total[:, one], func=ACT.Sqrt, scale=1.0 / LATENT, bias=eps[:]
-                    )
 
-        def normalise():
-            staged = []
-            for j in range(TOKENS // PAIR):
-                h_pair = h_pool.tile([P, 2, LATENT], BF16, name="h_pair", tag="h_pair")
-                for x in range(2):
-                    b = 2 * j + x
-                    one = slice(b, b + 1)
-                    nc.vector.reciprocal(out=inv_rms[:, one], in_=rms[:, one])
-                    nc.vector.scalar_tensor_tensor(
-                        out=h_pair[:, x, :],
-                        in0=latent[:, b, :],
-                        scalar=inv_rms[:, one],
-                        in1=gain[:],
-                        op0=ALU.mult,
-                        op1=ALU.mult,
-                    )
-                staged.append([copy_out(bank) for bank in transpose_pair(h_pair, PASSES_B, acc_pool, "acc", WOVEN_B)])
-            for j in range(TOKENS // PAIR):
-                quantise_activations(staged[j], j, h_codes, h_scales)
-
-        nope_out = out_0.rearrange("(b p) h x -> p b (h x)", p=P)
+        nope_out = out_0.rearrange("(b p) h x -> p b h x", p=P)
         rope_out = out_1.rearrange("(b p) h j -> p b (h j)", p=P)
+        q_tiles = {}
 
-        def query_tiles(second):
-            n_nope = 1 if second else 3
-            nope_sb = out_pool.tile([P, TOKEN_BLOCKS, n_nope, NOPE], F32, name="nope_sb", tag="nope_sb")
-            rope_sb = out_pool.tile([P, TOKEN_BLOCKS, 2, ROPE], F32, name="rope_sb", tag="rope_sb")
-            return nope_sb, rope_sb
-
-        def query_columns(second, blocks, nope_sb, rope_sb, w_codes, w_scales):
-            width = PAIR if second else BANK
-            for b in blocks:
-                acc = acc_pool.tile([P, BANK], F32, name="acc", tag="acc")
-                multiply(acc[:, 0:width], h_codes, h_scales, b, w_codes, w_scales, PASSES_B)
-                by_head = acc[:, 0 : 2 * HEAD].rearrange("p (h x) -> p h x", x=HEAD)
-                if second:
-                    nc.scalar.copy(out=rope_sb[:, b, :, :], in_=by_head[:, :, 0:ROPE])
-                    nc.scalar.copy(out=nope_sb[:, b, 0, :], in_=acc[:, ROPE:HEAD])
-                else:
-                    nc.scalar.copy(out=rope_sb[:, b, :, :], in_=by_head[:, :, NOPE:HEAD])
-                    nc.scalar.copy(out=nope_sb[:, b, 0:2, :], in_=by_head[:, :, 0:NOPE])
-                    nc.scalar.copy(out=nope_sb[:, b, 2, :], in_=acc[:, 2 * HEAD : BANK])
-
-        def store_unrotated(m, second, nope_sb):
-            first_nope = NOPE * (4 * m + 3 * second)
+        def finish_query(n, b):
+            if b == 0:
+                q_tiles[n] = q_pool.tile([P, TOKEN_BLOCKS, Q_WIDTH], F32, name="q_sb", tag="q_sb")
+            q_sb = q_tiles[n]
+            nc.scalar.copy(
+                out=q_sb[:, b, 0:GROUP].rearrange("t (p r) -> t p r", r=ROWS), in_=natural(accs[("b", n, b)][:])
+            )
+            first_head = -(-GROUP * n // HEAD)
+            start = HEAD * first_head - GROUP * n
+            count = 2 if n % 3 else 3
             nc.sync.dma_start(
-                out=nope_out[:, :, first_nope : first_nope + NOPE * nope_sb.shape[2]],
-                in_=nope_sb[:].rearrange("p b h x -> p b (h x)"),
+                out=nope_out[:, b, first_head : first_head + count, :],
+                in_=q_sb[:, b, start : start + HEAD * count].rearrange("t (h x) -> t h x", x=HEAD)[:, :, 0:NOPE],
             )
 
-        def rotate(m, second, rope_sb, engine):
-            shape = [P, TOKEN_BLOCKS, 2, ROPE]
-            straight = out_pool.tile(shape, F32, name="straight", tag="straight")
-            engine.tensor_tensor(
-                out=straight[:], in0=rope_sb[:], in1=cos_sb[:].unsqueeze(2).to_broadcast(shape), op=ALU.mult
+        def store_split_head(n):
+            if n % 3 == 0:
+                return
+            col = 448 if n % 3 == 1 else 0
+            head = (GROUP * n + col) // HEAD
+            within = GROUP * n + col - HEAD * head
+            nc.sync.dma_start(
+                out=nope_out[:, :, head, within : within + 64],
+                in_=q_tiles[n][:, :, col : col + 64],
             )
-            crossed = out_pool.tile(shape, F32, name="crossed", tag="crossed")
-            engine.tensor_tensor(
-                out=crossed[:], in0=rope_sb[:], in1=sin_swapped[:].unsqueeze(2).to_broadcast(shape), op=ALU.mult
+
+        def rotate(n, blocks):
+            first = (NOPE - GROUP * n) % HEAD
+            count = 3 if n % 3 else 2
+            shape = [P, blocks.stop - blocks.start, count, ROPE]
+            rope = q_tiles[n][:, blocks, first : first + HEAD * count].rearrange("t b (h x) -> t b h x", x=HEAD)[:, :, :, 0:ROPE]
+            straight = rope_pool.tile(shape, F32, name="straight", tag="straight")
+            nc.vector.tensor_tensor(
+                out=straight[:], in0=rope, in1=cos_sb[:, blocks, :].unsqueeze(2).to_broadcast(shape), op=ALU.mult
             )
-            rotated = out_pool.tile(shape, F32, name="rotated", tag="rotated")
-            engine.tensor_tensor(
+            crossed = rope_pool.tile(shape, F32, name="crossed", tag="crossed")
+            nc.vector.tensor_tensor(
+                out=crossed[:], in0=rope, in1=sin_swapped[:, blocks, :].unsqueeze(2).to_broadcast(shape), op=ALU.mult
+            )
+            rotated = out_pool.tile(shape, F32, name="rotated", tag="rotated%d" % shape[1], bufs=2 if shape[1] == TOKEN_BLOCKS else 4)
+            nc.vector.tensor_tensor(
                 out=rotated[:, :, :, low], in0=straight[:, :, :, low], in1=crossed[:, :, :, high], op=ALU.add
             )
-            engine.tensor_tensor(
+            nc.vector.tensor_tensor(
                 out=rotated[:, :, :, high], in0=straight[:, :, :, high], in1=crossed[:, :, :, low], op=ALU.add
             )
-            first_rope = ROPE * (4 * m + 2 * second)
+            head = (GROUP * n + first) // HEAD
             nc.sync.dma_start(
-                out=rope_out[:, :, first_rope : first_rope + 2 * ROPE],
+                out=rope_out[:, blocks, ROPE * head : ROPE * (head + count)],
                 in_=rotated[:].rearrange("p b h j -> p b (h j)"),
             )
 
-        groups = [
-            (2 * c + (len(pairs_x) if c > 0 else 0), 2, PASSES_A, factors_a, 4 * c, None) for c in range(n_groups_a)
-        ]
-        for m in range(HEADS // 4):
-            groups.append((first_b + 3 * m, 2, PASSES_B, factors_b, 6 * m, WOVEN_B))
-            groups.append((first_b + 3 * m + 2, 1, PASSES_B, factors_b, 6 * m + 4, WOVEN_B))
+        singles = []
+        for g in range(PASSES_A):
+            singles.append(("a", 0, g))
+            singles.append(("x", 0, g))
+        a_items = [("a", n, g) for n in range(1, GROUPS_A) for g in range(PASSES_A)]
+        b_items = [("b", n, g) for n in range(GROUPS_B) for g in range(PASSES_B)]
+        first, second = H_AT
+        steps = [[item] for item in singles]
+        for part in (a_items, b_items[0:first], [("h", 0, 0)], b_items[first:second], [("h", 1, 0)], b_items[second:]):
+            together = TOGETHER if part[0] == b_items[second] else 1
+            steps.extend([part[j : j + together] for j in range(0, len(part), together)])
+        place = {}
+        for i in range(len(steps)):
+            for item in steps[i]:
+                place[item] = i
 
-        steps = []
-        for i in range(len(groups)):
-            for j in range(groups[i][1]):
-                share = TOKEN_BLOCKS // groups[i][1]
-                steps.append((i, j, range(share * j, share * (j + 1))))
-        weights = {}
-        results = {}
-        waiting = []
-        for s in range(len(steps) + LAG):
-            if s < len(steps):
-                i, j, blocks = steps[s]
-                if j == 0:
-                    weights[i] = weight_tiles(*groups[i])
-                quantise_weights(j, *weights[i], *groups[i])
-            if s == 1:
-                quantise_hidden_states()
-            if len(waiting) > 0 and (waiting[0][0] < s or s >= len(steps)):
-                rotate(*waiting[0][1])
-                waiting = waiting[1:]
-            if s >= LAG:
-                i, j, blocks = steps[s - LAG]
-                last = j == groups[i][1] - 1
-                if i < n_groups_a:
-                    latent_columns(i, blocks, *weights[i])
-                    if last and i == n_groups_a - 1:
-                        normalise()
+        products = []
+        for kind, n_groups, passes in (("a", GROUPS_A, PASSES_A), ("b", GROUPS_B, PASSES_B)):
+            for n in range(n_groups):
+                order = [(b, g) for b in range(TOKEN_BLOCKS) for g in range(passes)]
+                if (kind, n) == ("a", 0):
+                    order = [(b, g) for g in range(passes) for b in range(TOKEN_BLOCKS)]
+                products.extend([(kind, n, b, g, passes) for b, g in order])
+
+        def needs(product):
+            kind, n, b, g, passes = product
+            act = ("x", 0, g) if kind == "a" else ("h", b // 2, 0)
+            return max(place[(kind, n, g)], place[act])
+
+        for i in range(AHEAD):
+            for item in steps[i]:
+                prescale(item)
+        closed = []
+        live = 0
+        rotations = []
+        done = 0
+        i = 0
+        while done < len(products) or len(closed) > 0 or len(rotations) > 0:
+            if i == 3:
+                spread_gain()
+            for kind, n, b in closed:
+                if kind == "a":
+                    finish_latent(n, b)
                 else:
-                    m, second = divmod(i - n_groups_a, 2)
-                    if j == 0:
-                        results[i] = query_tiles(second)
-                    query_columns(second, blocks, *results[i], *weights[i])
-                    if last:
-                        store_unrotated(m, second, results[i][0])
-                        waiting.append((s, (m, second, results[i][1], nc.vector)))
-        for late in waiting:
-            rotate(*late[1])
+                    finish_query(n, b)
+            if i < len(steps):
+                for item in steps[i]:
+                    transposes(item)
+                for item in steps[i]:
+                    copies_out(item)
+            if 1 <= i <= len(steps):
+                for item in steps[i - 1]:
+                    quantises(item)
+            if i + AHEAD < len(steps):
+                for item in steps[i + AHEAD]:
+                    prescale(item)
+            for n, b in rotations:
+                rotate(n, b)
+            rotations = []
+            for kind, n, b in closed:
+                if (kind, n) == ("a", GROUPS_A - 1):
+                    normalise(b)
+                if kind == "b":
+                    if b == TOKEN_BLOCKS - 1:
+                        store_split_head(n)
+                    if n == GROUPS_B - 1:
+                        rotations.append((n, slice(b, b + 1)))
+                    elif b == TOKEN_BLOCKS - 1:
+                        rotations.append((n, slice(0, TOKEN_BLOCKS)))
+            live -= len(closed)
+            closed = []
+            budget = (BUDGET_A if i < place[("h", 0, 0)] else BUDGET_B)
+            slack = 2 if i < len(steps) else 1
+            while done < len(products) and budget > 0 and needs(products[done]) <= i - slack:
+                kind, n, b, g, passes = products[done]
+                if g == 0 and live == 4:
+                    break
+                if g == 0:
+                    live += 1
+                multiply(kind, n, b, g, passes)
+                if g == passes - 1:
+                    closed.append((kind, n, b))
+                done += 1
+                budget -= 1
+            i += 1

@@ -29,15 +29,21 @@ PASSES_B = LATENT // K_PASS
 GROUPS_A = LATENT // GROUP
 GROUPS_B = HEADS * HEAD // GROUP
 TOKEN_BLOCKS = TOKENS // P
-HALF = HIDDEN // 2
 FLOPS = 2 * TOKENS * HIDDEN * LATENT + 2 * TOKENS * LATENT * HEADS * HEAD
-H_AT = (5, 7)
+
 RAW_BUFS = {1: 2, 2: 7, 3: 3}
-TOGETHER = 1
+UNITS = GROUP // ROPE
+SETS = ((0, 1), (2, 3), (4,), (5,))
+SET_UNITS = 11
+SET_HEADS = 5
+H_AT = (5, 7)
+AHEAD = 2
+SETUP_AT = 5
+SLACK = 2
 BUDGET_A = 4
 BUDGET_B = 6
-AHEAD = 2
-Q_WIDTH = 640
+TOGETHER = 1
+ACCS = 4
 
 
 def tile_deepseekv3attention_pa_kernel(
@@ -48,56 +54,55 @@ def tile_deepseekv3attention_pa_kernel(
         keep = ctx.enter_context(tc.tile_pool(name="keep", bufs=1))
         raw_pool = ctx.enter_context(tc.tile_pool(name="raw_pool", bufs=1))
         grouped_pool = ctx.enter_context(tc.tile_pool(name="grouped_pool", bufs=4))
-        weight_pool = ctx.enter_context(tc.tile_pool(name="weight_pool", bufs=16))
+        weight_pool = ctx.enter_context(tc.tile_pool(name="weight_pool", bufs=14))
         h_pool = ctx.enter_context(tc.tile_pool(name="h_pool", bufs=3))
         q_pool = ctx.enter_context(tc.tile_pool(name="q_pool", bufs=3))
         rope_pool = ctx.enter_context(tc.tile_pool(name="rope_pool", bufs=1))
         out_pool = ctx.enter_context(tc.tile_pool(name="out_pool", bufs=2))
-        bank_pool = ctx.enter_context(tc.psum_pool(name="bank_pool", bufs=4))
-        acc_pool = ctx.enter_context(tc.psum_pool(name="acc_pool", bufs=4))
+        bank_pool = ctx.enter_context(tc.psum_pool(name="bank_pool", bufs=8 - ACCS))
+        acc_pool = ctx.enter_context(tc.psum_pool(name="acc_pool", bufs=ACCS))
         ctx.enter_context(tc.manual_schedule())
 
-        n_a = sq_a.shape[0] * sq_a.shape[1]
-        n_b = sq_b.shape[0] * sq_b.shape[1]
-        row_zero = grouped_pool.tile([P, GROUP + LATENT], BF16, name="grouped", tag="grouped", align_bytes=64)
-        nc.vector.memset(row_zero[:], 0.0)
-        nc.sync.dma_start(out=row_zero[0:1, 0:n_a], in_=sq_a.rearrange("a b -> (a b)").unsqueeze(0))
-        nc.sync.dma_start(
-            out=row_zero[0:1, n_a : n_a + n_b], in_=sq_b.rearrange("a b -> (a b)").unsqueeze(0)
-        )
+        sq_rows = keep.tile([P, sq_a.shape[1] + sq_b.shape[1]], BF16)
+        nc.vector.memset(sq_rows[:], 0.0)
+        nc.sync.dma_start(out=sq_rows[0 : sq_a.shape[0], 0 : sq_a.shape[1]], in_=sq_a)
+        nc.sync.dma_start(out=sq_rows[0 : sq_b.shape[0], sq_a.shape[1] :], in_=sq_b)
+        gain_row = h_pool.tile([P, LATENT], BF16, name="h_row", tag="h_row")
+        nc.vector.memset(gain_row[:], 0.0)
         cos_bf = keep.tile([P, TOKEN_BLOCKS, ROPE], BF16)
         sin_bf = keep.tile([P, TOKEN_BLOCKS, ROPE], BF16)
 
         def load_small():
-            nc.sync.dma_start(out=row_zero[0:1, GROUP : GROUP + LATENT], in_=q_ln_w.unsqueeze(0))
+            nc.sync.dma_start(out=gain_row[0:1, :], in_=q_ln_w.unsqueeze(0))
             nc.sync.dma_start(out=cos_bf[:], in_=cos.rearrange("(b p) j -> p b j", p=P))
             nc.sync.dma_start(out=sin_bf[:], in_=sin.rearrange("(b p) j -> p b j", p=P))
-
-        rows_x = hidden_states.rearrange("(b p) k -> p b k", p=P)
-
-        def weight_rows(weights, n):
-            return weights[GROUP * n : GROUP * (n + 1), :].rearrange("(p r) k -> p r k", r=ROWS)
 
         raw = {}
 
         def load(kind, n, first, count):
-            rows = rows_x if kind == "x" else weight_rows(wq_a if kind == "a" else wq_b, n)
             tag = "raw_%d" % count
             tile = raw_pool.tile([P, ROWS, K_PASS * count], BF16, name=tag, tag=tag, bufs=RAW_BUFS[count])
-            nc.sync.dma_start(out=tile[:], in_=rows[:, :, K_PASS * first : K_PASS * (first + count)])
+            cols = slice(K_PASS * first, K_PASS * (first + count))
+            if kind == "x":
+                rows = hidden_states.rearrange("(b p) k -> p b k", p=P)
+            else:
+                weights = wq_a if kind == "a" else wq_b
+                rows = weights[GROUP * n : GROUP * (n + 1), :].rearrange("(p r) k -> p r k", r=ROWS)
+            nc.sync.dma_start(out=tile[:], in_=rows[:, :, cols])
             for g in range(count):
                 raw[(kind, n, first + g)] = tile[:, :, K_PASS * g : K_PASS * (g + 1)]
 
-        loads = []
-        loads.extend([("a", 0, 0, 1), ("x", 0, 0, 2), ("a", 0, 1, 1), ("a", 0, 2, 2), ("x", 0, 2, 2)])
+        load("a", 0, 0, 1)
+        load("x", 0, 0, 2)
+        load_small()
+        load("a", 0, 1, 1)
+        load("a", 0, 2, 2)
+        load("x", 0, 2, 2)
         for n in range(1, GROUPS_A):
-            loads.extend([("a", n, g, 2) for g in range(0, PASSES_A, 2)])
-        for n in range(GROUPS_B):
-            loads.append(("b", n, 0, PASSES_B))
-        for i in range(len(loads)):
-            load(*loads[i])
-            if i == 3:
-                load_small()
+            for g in range(0, PASSES_A, 2):
+                load("a", n, g, 2)
+        for n in range(RAW_BUFS[PASSES_B]):
+            load("b", n, 0, PASSES_B)
 
         ident = keep.tile([P, P], F32)
         masks.make_identity(nc, ident[:])
@@ -108,30 +113,29 @@ def tile_deepseekv3attention_pa_kernel(
         warm = keep.tile([P, 1], F32)
         nc.scalar.activation(out=warm[:], in_=eps[:], func=ACT.Sqrt)
 
-        def spread(n):
-            bank = bank_pool.tile([P, GROUP], F32, name="bank", tag="bank")
-            nc.tensor.matmul(
-                out=bank[:], lhsT=ones[:], rhs=row_zero[:, GROUP * n : GROUP * (n + 1)], start=True, stop=True
-            )
-            return bank
-
-        bank = spread(0)
+        select = keep.tile([P, GROUPS_B, P], BF16)
+        nc.vector.tensor_copy(
+            out=select[:].rearrange("p n (q i) -> p (n q) i", i=32),
+            in_=ident[:, 0 : 4 * GROUPS_B].unsqueeze(2).to_broadcast([P, 4 * GROUPS_B, 32]),
+        )
         factors = {}
-        for kind, first, shape in (("a", 0, sq_a.shape), ("b", n_a, sq_b.shape)):
-            table = keep.tile([P, shape[0] // 4, shape[1]], F32, name="factors_" + kind)
-            by_quarter = bank[:, first : first + shape[0] * shape[1]].rearrange(
-                "p (n q c) -> p n q c", q=4, c=shape[1]
-            )
-            for quarter in range(4):
-                rows = slice(32 * quarter, 32 * (quarter + 1))
-                nc.scalar.copy(out=table[rows, :, :], in_=by_quarter[rows, :, quarter, :])
-            factors[kind] = table
+
+        def factor_table(kind, groups, first, width):
+            bank = bank_pool.tile([P, groups, width], F32, name="bank", tag="bank")
+            for n in range(groups):
+                nc.tensor.matmul(
+                    out=bank[:, n, :],
+                    lhsT=select[:, n, :],
+                    rhs=sq_rows[:, first : first + width],
+                    start=True,
+                    stop=True,
+                )
+            factors[kind] = keep.tile([P, groups, width], F32, name="factors_" + kind)
+            nc.scalar.copy(out=factors[kind][:], in_=bank[:])
+
+        factor_table("a", GROUPS_A, 0, sq_a.shape[1])
+
         gain = keep.tile([P, LATENT], F32)
-
-        def spread_gain():
-            for n in range(LATENT // GROUP):
-                nc.scalar.copy(out=gain[:, GROUP * n : GROUP * (n + 1)], in_=spread(1 + n)[:])
-
         half_rope = ROPE // 2
         low = slice(0, half_rope)
         high = slice(half_rope, ROPE)
@@ -142,6 +146,14 @@ def tile_deepseekv3attention_pa_kernel(
         nc.gpsimd.tensor_scalar(
             out=sin_swapped[:, :, high], in0=sin_bf[:, :, low], scalar1=-1.0, scalar2=0.0, op0=ALU.mult, op1=ALU.add
         )
+
+        def setup():
+            factor_table("b", GROUPS_B, sq_a.shape[1], sq_b.shape[1])
+            for n in range(LATENT // GROUP):
+                cols = slice(GROUP * n, GROUP * (n + 1))
+                bank = bank_pool.tile([P, GROUP], F32, name="bank", tag="bank")
+                nc.tensor.matmul(out=bank[:], lhsT=ones[:], rhs=gain_row[:, cols], start=True, stop=True)
+                nc.scalar.copy(out=gain[:, cols], in_=bank[:])
 
         banks = {}
         grouped = {}
@@ -157,16 +169,14 @@ def tile_deepseekv3attention_pa_kernel(
                         out=block, in0=block, scalar1=factors[kind][:, n, 4 * g + c : 4 * g + c + 1]
                     )
 
-        def transpose_rows(rows, n_rows):
-            result = []
-            for pair in range(n_rows // 2):
-                bank = bank_pool.tile([P, 2, 2 * P], F32, name="bank", tag="bank")
-                for u in range(2):
-                    for x in range(2):
-                        words = rows[:, 2 * pair + x, :].bitcast(F32)[:, P * u : P * (u + 1)]
-                        nc.tensor.transpose(bank[:, u, P * x : P * (x + 1)], words, ident[:])
-                result.append(bank)
-            return result
+        def transpose_pair(rows):
+            bank = bank_pool.tile([P, 2, 2 * P], F32, name="bank", tag="bank")
+            for u in range(2):
+                for x in range(2):
+                    nc.tensor.transpose(
+                        bank[:, u, P * x : P * (x + 1)], rows[x].bitcast(F32)[:, P * u : P * (u + 1)], ident[:]
+                    )
+            return bank
 
         def copy_out(some_banks):
             tile = grouped_pool.tile([P, 2 * P * len(some_banks), 4], BF16, name="grouped", tag="grouped", align_bytes=64)
@@ -193,16 +203,16 @@ def tile_deepseekv3attention_pa_kernel(
         def transposes(item):
             kind, n, g = item
             if kind == "h":
-                banks[item] = []
-                for g in range(PASSES_B):
-                    bank = bank_pool.tile([P, 2, 2 * P], F32, name="bank", tag="bank")
-                    for u in range(2):
-                        for x in range(2):
-                            words = h_rows[2 * n + x][:].bitcast(F32)[:, 2 * P * g + P * u : 2 * P * g + P * (u + 1)]
-                            nc.tensor.transpose(bank[:, u, P * x : P * (x + 1)], words, ident[:])
-                    banks[item].append(bank)
+                banks[item] = [
+                    transpose_pair([h_rows[2 * n + x][:, K_PASS * c : K_PASS * (c + 1)] for x in range(2)])
+                    for c in range(PASSES_B)
+                ]
             else:
-                banks[item] = transpose_rows(raw[item], ROWS)
+                banks[item] = [
+                    transpose_pair([raw[item][:, 2 * pair + x, :] for x in range(2)]) for pair in range(ROWS // 2)
+                ]
+                if kind == "b" and g == PASSES_B - 1 and n + RAW_BUFS[PASSES_B] < GROUPS_B:
+                    load("b", n + RAW_BUFS[PASSES_B], 0, PASSES_B)
 
         def copies_out(item):
             if item[0] == "h":
@@ -214,16 +224,14 @@ def tile_deepseekv3attention_pa_kernel(
             kind, n, g = item
             if kind == "h":
                 cols = slice(2 * P * n, 2 * P * (n + 1))
-                for g in range(PASSES_B):
-                    quantise(grouped[item][g], h_codes[:, g, cols], h_scales[:, g, cols])
+                for c in range(PASSES_B):
+                    quantise(grouped[item][c], h_codes[:, c, cols], h_scales[:, c, cols])
             elif kind == "x":
                 quantise(grouped[item][0], x_codes[:, g, :], x_scales[:, g, :])
             else:
-                w_codes = weight_pool.tile([P, GROUP], U32, name="w_codes", tag="w_codes", align_bytes=64)
-                w_scales = weight_pool.tile([P, GROUP], U8, name="w_scales", tag="w_scales", align_bytes=64)
-                quantise(grouped[item][0], w_codes[:], w_scales[:])
-                codes[item] = w_codes
-                scales[item] = w_scales
+                codes[item] = weight_pool.tile([P, GROUP], U32, name="w_codes", tag="w_codes", align_bytes=64)
+                scales[item] = weight_pool.tile([P, GROUP], U8, name="w_scales", tag="w_scales", align_bytes=64)
+                quantise(grouped[item][0], codes[item][:], scales[item][:])
 
         accs = {}
 
@@ -242,7 +250,7 @@ def tile_deepseekv3attention_pa_kernel(
                 stop=(g == passes - 1),
             )
 
-        def natural(columns):
+        def in_order(columns):
             return columns.rearrange("t (r p) -> t p r", r=ROWS)
 
         def finish_latent(c, b):
@@ -254,7 +262,7 @@ def tile_deepseekv3attention_pa_kernel(
                 latents[c] = q_pool.tile([P, TOKEN_BLOCKS, GROUP], F32, name="q_sb", tag="q_sb")
             nc.vector.tensor_tensor(
                 out=latents[c][:, b, :].rearrange("t (p r) -> t p r", r=ROWS),
-                in0=natural(acc[:]),
+                in0=in_order(acc[:]),
                 in1=gain[:, cols].rearrange("t (p r) -> t p r", r=ROWS),
                 op=ALU.mult,
             )
@@ -275,61 +283,79 @@ def tile_deepseekv3attention_pa_kernel(
                     out=h_rows[b][:, GROUP * c : GROUP * (c + 1)], in0=latents[c][:, b, :], scalar1=inv_rms[:, one]
                 )
 
-        nope_out = out_0.rearrange("(b p) h x -> p b h x", p=P)
+        nope_out = out_0.rearrange("(b p) h x -> p b (h x)", p=P)
         rope_out = out_1.rearrange("(b p) h j -> p b (h j)", p=P)
-        q_tiles = {}
+        nope_tiles = {}
+        rope_tiles = {}
+        partial = {}
+
+        def unrotated_before(unit):
+            return unit - unit // 3
+
+        def rotated_before(unit):
+            return (unit + 0) // 3
+
+        def first_group(n):
+            return [s for s in SETS if n in s][0][0]
 
         def finish_query(n, b):
-            if b == 0:
-                q_tiles[n] = q_pool.tile([P, TOKEN_BLOCKS, Q_WIDTH], F32, name="q_sb", tag="q_sb")
-            q_sb = q_tiles[n]
-            nc.scalar.copy(
-                out=q_sb[:, b, 0:GROUP].rearrange("t (p r) -> t p r", r=ROWS), in_=natural(accs[("b", n, b)][:])
-            )
-            first_head = -(-GROUP * n // HEAD)
-            start = HEAD * first_head - GROUP * n
-            count = 2 if n % 3 else 3
-            nc.sync.dma_start(
-                out=nope_out[:, b, first_head : first_head + count, :],
-                in_=q_sb[:, b, start : start + HEAD * count].rearrange("t (h x) -> t h x", x=HEAD)[:, :, 0:NOPE],
-            )
-
-        def store_split_head(n):
-            if n % 3 == 0:
-                return
-            col = 448 if n % 3 == 1 else 0
-            head = (GROUP * n + col) // HEAD
-            within = GROUP * n + col - HEAD * head
-            nc.sync.dma_start(
-                out=nope_out[:, :, head, within : within + 64],
-                in_=q_tiles[n][:, :, col : col + 64],
-            )
-
-        def rotate(n, blocks):
-            first = (NOPE - GROUP * n) % HEAD
-            count = 3 if n % 3 else 2
-            shape = [P, blocks.stop - blocks.start, count, ROPE]
-            rope = q_tiles[n][:, blocks, first : first + HEAD * count].rearrange("t b (h x) -> t b h x", x=HEAD)[:, :, :, 0:ROPE]
-            straight = rope_pool.tile(shape, F32, name="straight", tag="straight")
-            nc.vector.tensor_tensor(
-                out=straight[:], in0=rope, in1=cos_sb[:, blocks, :].unsqueeze(2).to_broadcast(shape), op=ALU.mult
-            )
-            crossed = rope_pool.tile(shape, F32, name="crossed", tag="crossed")
-            nc.vector.tensor_tensor(
-                out=crossed[:], in0=rope, in1=sin_swapped[:, blocks, :].unsqueeze(2).to_broadcast(shape), op=ALU.mult
-            )
-            rotated = out_pool.tile(shape, F32, name="rotated", tag="rotated%d" % shape[1], bufs=2 if shape[1] == TOKEN_BLOCKS else 4)
-            nc.vector.tensor_tensor(
-                out=rotated[:, :, :, low], in0=straight[:, :, :, low], in1=crossed[:, :, :, high], op=ALU.add
-            )
-            nc.vector.tensor_tensor(
-                out=rotated[:, :, :, high], in0=straight[:, :, :, high], in1=crossed[:, :, :, low], op=ALU.add
-            )
-            head = (GROUP * n + first) // HEAD
-            nc.sync.dma_start(
-                out=rope_out[:, blocks, ROPE * head : ROPE * (head + count)],
-                in_=rotated[:].rearrange("p b h j -> p b (h j)"),
-            )
+            unit_0 = UNITS * first_group(n)
+            if b == 0 and n == first_group(n):
+                nope_tiles[n] = q_pool.tile([P, TOKEN_BLOCKS, SET_UNITS, ROPE], F32, name="q_sb", tag="q_sb")
+                rope_tiles[n] = out_pool.tile([P, TOKEN_BLOCKS, SET_HEADS, ROPE], F32, name="rotated", tag="rotated")
+            by_unit = accs[("b", n, b)][:].rearrange("t (r s q) -> t s q r", r=ROWS, s=UNITS)
+            nope = nope_tiles[first_group(n)]
+            for kind in range(3):
+                first = (kind - UNITS * n) % 3
+                columns = by_unit[:, first:UNITS:3, :, :]
+                count = columns.shape[1]
+                if kind < 2:
+                    at = unrotated_before(UNITS * n + first) - unrotated_before(unit_0)
+                    nc.scalar.copy(
+                        out=nope[:, b, at : at + 2 * count - 1 : 2, :].rearrange("t s (q r) -> t s q r", r=ROWS),
+                        in_=columns,
+                    )
+                else:
+                    if b == 0:
+                        partial[n] = [
+                            rope_pool.tile([P, TOKEN_BLOCKS, count, ROPE], F32, name=name, tag=name)
+                            for name in ("straight", "crossed")
+                        ]
+                    for product, table in zip(partial[n], (cos_sb, sin_swapped)):
+                        nc.vector.tensor_tensor(
+                            out=product[:, b, :, :].rearrange("t s (q r) -> t s q r", r=ROWS),
+                            in0=columns,
+                            in1=table[:, b, :]
+                            .rearrange("t (q r) -> t q r", r=ROWS)
+                            .unsqueeze(1)
+                            .to_broadcast([P, count, ROPE // ROWS, ROWS]),
+                            op=ALU.mult,
+                        )
+            alone = n == GROUPS_B - 1
+            blocks = slice(b, b + 1) if alone else slice(0, TOKEN_BLOCKS)
+            if alone or b == TOKEN_BLOCKS - 1:
+                straight, crossed = partial[n]
+                at = rotated_before(UNITS * n) - rotated_before(unit_0)
+                heads = slice(at, at + straight.shape[2])
+                rotated = rope_tiles[first_group(n)]
+                for half, other in ((low, high), (high, low)):
+                    nc.vector.tensor_tensor(
+                        out=rotated[:, blocks, heads, half],
+                        in0=straight[:, blocks, :, half],
+                        in1=crossed[:, blocks, :, other],
+                        op=ALU.add,
+                    )
+                if n == [s for s in SETS if n in s][0][-1]:
+                    end = UNITS * (n + 1)
+                    for out, tile, before in (
+                        (nope_out, nope, unrotated_before),
+                        (rope_out, rotated, rotated_before),
+                    ):
+                        width = before(end) - before(unit_0)
+                        nc.sync.dma_start(
+                            out=out[:, blocks, ROPE * before(unit_0) : ROPE * before(end)],
+                            in_=tile[:, blocks, 0:width, :].rearrange("p b s j -> p b (s j)"),
+                        )
 
         singles = []
         for g in range(PASSES_A):
@@ -365,12 +391,11 @@ def tile_deepseekv3attention_pa_kernel(
                 prescale(item)
         closed = []
         live = 0
-        rotations = []
         done = 0
         i = 0
-        while done < len(products) or len(closed) > 0 or len(rotations) > 0:
-            if i == 3:
-                spread_gain()
+        while done < len(products) or len(closed) > 0:
+            if i == SETUP_AT:
+                setup()
             for kind, n, b in closed:
                 if kind == "a":
                     finish_latent(n, b)
@@ -387,26 +412,16 @@ def tile_deepseekv3attention_pa_kernel(
             if i + AHEAD < len(steps):
                 for item in steps[i + AHEAD]:
                     prescale(item)
-            for n, b in rotations:
-                rotate(n, b)
-            rotations = []
             for kind, n, b in closed:
                 if (kind, n) == ("a", GROUPS_A - 1):
                     normalise(b)
-                if kind == "b":
-                    if b == TOKEN_BLOCKS - 1:
-                        store_split_head(n)
-                    if n == GROUPS_B - 1:
-                        rotations.append((n, slice(b, b + 1)))
-                    elif b == TOKEN_BLOCKS - 1:
-                        rotations.append((n, slice(0, TOKEN_BLOCKS)))
             live -= len(closed)
             closed = []
-            budget = (BUDGET_A if i < place[("h", 0, 0)] else BUDGET_B)
-            slack = 2 if i < len(steps) else 1
+            budget = BUDGET_A if i < place[("h", 0, 0)] else BUDGET_B
+            slack = SLACK if i < len(steps) else 1
             while done < len(products) and budget > 0 and needs(products[done]) <= i - slack:
                 kind, n, b, g, passes = products[done]
-                if g == 0 and live == 4:
+                if g == 0 and live == ACCS:
                     break
                 if g == 0:
                     live += 1

@@ -31,15 +31,19 @@ GROUPS_B = HEADS * HEAD // GROUP
 TOKEN_BLOCKS = TOKENS // P
 FLOPS = 2 * TOKENS * HIDDEN * LATENT + 2 * TOKENS * LATENT * HEADS * HEAD
 
-RAW_BUFS = {1: 2, 2: 7, 3: 3}
+RAW_BUFS = {1: 2, 2: 5, 3: 3}
 UNITS = GROUP // ROPE
 SETS = ((0, 1), (2, 3), (4,), (5,))
 SET_UNITS = 11
 SET_HEADS = 5
 H_AT = (5, 7)
+LOADS = [("a", 0, 0, 1), ("x", 0, 0, 2), (), ("a", 0, 1, 1), ("a", 0, 2, 2), ("x", 0, 2, 2), ("a", 1, 0, 2), ("a", 1, 2, 2), ("a", 2, 0, 2), ("a", 2, 2, 2)]
+STEPS_A = [("a", 0, 0), ("x", 0, 0), ("a", 0, 1), ("x", 0, 1), ("a", 0, 2), ("x", 0, 2), ("a", 0, 3), ("x", 0, 3)] + [("a", n, g) for n in (1, 2) for g in range(4)]
+SCALED_BUFS = 4
 AHEAD = 2
 SETUP_AT = 5
 SLACK = 2
+PART = 2
 BUDGET_A = 4
 BUDGET_B = 6
 TOGETHER = 1
@@ -53,6 +57,7 @@ def tile_deepseekv3attention_pa_kernel(
     with ExitStack() as ctx:
         keep = ctx.enter_context(tc.tile_pool(name="keep", bufs=1))
         raw_pool = ctx.enter_context(tc.tile_pool(name="raw_pool", bufs=1))
+        scaled_pool = ctx.enter_context(tc.tile_pool(name="scaled_pool", bufs=SCALED_BUFS))
         grouped_pool = ctx.enter_context(tc.tile_pool(name="grouped_pool", bufs=4))
         weight_pool = ctx.enter_context(tc.tile_pool(name="weight_pool", bufs=14))
         h_pool = ctx.enter_context(tc.tile_pool(name="h_pool", bufs=3))
@@ -92,15 +97,11 @@ def tile_deepseekv3attention_pa_kernel(
             for g in range(count):
                 raw[(kind, n, first + g)] = tile[:, :, K_PASS * g : K_PASS * (g + 1)]
 
-        load("a", 0, 0, 1)
-        load("x", 0, 0, 2)
-        load_small()
-        load("a", 0, 1, 1)
-        load("a", 0, 2, 2)
-        load("x", 0, 2, 2)
-        for n in range(1, GROUPS_A):
-            for g in range(0, PASSES_A, 2):
-                load("a", n, g, 2)
+        for args in LOADS:
+            if args:
+                load(*args)
+            else:
+                load_small()
         for n in range(RAW_BUFS[PASSES_B]):
             load("b", n, 0, PASSES_B)
 
@@ -163,11 +164,17 @@ def tile_deepseekv3attention_pa_kernel(
         def prescale(item):
             kind, n, g = item
             if kind in factors:
+                scaled = scaled_pool.tile([P, ROWS, K_PASS], BF16, name="scaled", tag="scaled")
                 for c in range(ROWS):
-                    block = raw[item][:, :, P * c : P * (c + 1)]
+                    cols = slice(P * c, P * (c + 1))
                     nc.vector.tensor_scalar_mul(
-                        out=block, in0=block, scalar1=factors[kind][:, n, 4 * g + c : 4 * g + c + 1]
+                        out=scaled[:, :, cols],
+                        in0=raw[item][:, :, cols],
+                        scalar1=factors[kind][:, n, 4 * g + c : 4 * g + c + 1],
                     )
+                raw[item] = scaled
+                if kind == "b" and g == PASSES_B - 1 and n + RAW_BUFS[PASSES_B] < GROUPS_B:
+                    load("b", n + RAW_BUFS[PASSES_B], 0, PASSES_B)
 
         def transpose_pair(rows):
             bank = bank_pool.tile([P, 2, 2 * P], F32, name="bank", tag="bank")
@@ -211,8 +218,6 @@ def tile_deepseekv3attention_pa_kernel(
                 banks[item] = [
                     transpose_pair([raw[item][:, 2 * pair + x, :] for x in range(2)]) for pair in range(ROWS // 2)
                 ]
-                if kind == "b" and g == PASSES_B - 1 and n + RAW_BUFS[PASSES_B] < GROUPS_B:
-                    load("b", n + RAW_BUFS[PASSES_B], 0, PASSES_B)
 
         def copies_out(item):
             if item[0] == "h":
@@ -298,6 +303,9 @@ def tile_deepseekv3attention_pa_kernel(
         def first_group(n):
             return [s for s in SETS if n in s][0][0]
 
+        def part_of(n):
+            return 1 if n == GROUPS_B - 1 else PART
+
         def finish_query(n, b):
             unit_0 = UNITS * first_group(n)
             if b == 0 and n == first_group(n):
@@ -316,14 +324,15 @@ def tile_deepseekv3attention_pa_kernel(
                         in_=columns,
                     )
                 else:
-                    if b == 0:
-                        partial[n] = [
-                            rope_pool.tile([P, TOKEN_BLOCKS, count, ROPE], F32, name=name, tag=name)
+                    part = part_of(n)
+                    if b % part == 0:
+                        partial[(n, b // part_of(n))] = [
+                            rope_pool.tile([P, part, count, ROPE], F32, name=name, tag=name, bufs=2)
                             for name in ("straight", "crossed")
                         ]
-                    for product, table in zip(partial[n], (cos_sb, sin_swapped)):
+                    for product, table in zip(partial[(n, b // part_of(n))], (cos_sb, sin_swapped)):
                         nc.vector.tensor_tensor(
-                            out=product[:, b, :, :].rearrange("t s (q r) -> t s q r", r=ROWS),
+                            out=product[:, b % part, :, :].rearrange("t s (q r) -> t s q r", r=ROWS),
                             in0=columns,
                             in1=table[:, b, :]
                             .rearrange("t (q r) -> t q r", r=ROWS)
@@ -331,18 +340,22 @@ def tile_deepseekv3attention_pa_kernel(
                             .to_broadcast([P, count, ROPE // ROWS, ROWS]),
                             op=ALU.mult,
                         )
-            alone = n == GROUPS_B - 1
-            blocks = slice(b, b + 1) if alone else slice(0, TOKEN_BLOCKS)
-            if alone or b == TOKEN_BLOCKS - 1:
-                straight, crossed = partial[n]
+
+        def store_query(n, b):
+            unit_0 = UNITS * first_group(n)
+            nope = nope_tiles[first_group(n)]
+            part = part_of(n)
+            blocks = slice(b + 1 - part, b + 1)
+            if (b + 1) % part == 0:
+                straight, crossed = partial[(n, b // part_of(n))]
                 at = rotated_before(UNITS * n) - rotated_before(unit_0)
                 heads = slice(at, at + straight.shape[2])
                 rotated = rope_tiles[first_group(n)]
                 for half, other in ((low, high), (high, low)):
                     nc.vector.tensor_tensor(
                         out=rotated[:, blocks, heads, half],
-                        in0=straight[:, blocks, :, half],
-                        in1=crossed[:, blocks, :, other],
+                        in0=straight[:, :, :, half],
+                        in1=crossed[:, :, :, other],
                         op=ALU.add,
                     )
                 if n == [s for s in SETS if n in s][0][-1]:
@@ -357,15 +370,12 @@ def tile_deepseekv3attention_pa_kernel(
                             in_=tile[:, blocks, 0:width, :].rearrange("p b s j -> p b (s j)"),
                         )
 
-        singles = []
-        for g in range(PASSES_A):
-            singles.append(("a", 0, g))
-            singles.append(("x", 0, g))
-        a_items = [("a", n, g) for n in range(1, GROUPS_A) for g in range(PASSES_A)]
+        a_items = []
+        singles = STEPS_A
         b_items = [("b", n, g) for n in range(GROUPS_B) for g in range(PASSES_B)]
         first, second = H_AT
         steps = [[item] for item in singles]
-        for part in (a_items, b_items[0:first], [("h", 0, 0)], b_items[first:second], [("h", 1, 0)], b_items[second:]):
+        for part in (b_items[0:first], [("h", 0, 0)], b_items[first:second], [("h", 1, 0)], b_items[second:]):
             together = TOGETHER if part[0] == b_items[second] else 1
             steps.extend([part[j : j + together] for j in range(0, len(part), together)])
         place = {}
@@ -415,6 +425,8 @@ def tile_deepseekv3attention_pa_kernel(
             for kind, n, b in closed:
                 if (kind, n) == ("a", GROUPS_A - 1):
                     normalise(b)
+                if kind == "b":
+                    store_query(n, b)
             live -= len(closed)
             closed = []
             budget = BUDGET_A if i < place[("h", 0, 0)] else BUDGET_B

@@ -33,16 +33,17 @@ FLOPS = 2 * TOKENS * HIDDEN * LATENT + 2 * TOKENS * LATENT * HEADS * HEAD
 
 RAW_BUFS = {1: 2, 2: 5, 3: 3}
 UNITS = GROUP // ROPE
-SETS = ((0, 1), (2, 3), (4,), (5,))
-SET_UNITS = 11
-SET_HEADS = 5
-H_AT = (5, 7)
-LOADS = [("a", 0, 0, 1), ("x", 0, 0, 2), (), ("a", 0, 1, 1), ("a", 0, 2, 2), ("x", 0, 2, 2), ("a", 1, 0, 2), ("a", 1, 2, 2), ("a", 2, 0, 2), ("a", 2, 2, 2)]
-STEPS_A = [("a", 0, 0), ("x", 0, 0), ("a", 0, 1), ("x", 0, 1), ("a", 0, 2), ("x", 0, 2), ("a", 0, 3), ("x", 0, 3)] + [("a", n, g) for n in (1, 2) for g in range(4)]
+H_AT = (6, 7)
+LOADS = [("a", 0, 0, 1), ("a", 0, 1, 1), ("a", 0, 2, 2), (), ("x", 0, 0, 2), ("a", 1, 0, 2), ("x", 0, 2, 2), ("a", 1, 2, 2), ("a", 2, 0, 2), ("a", 2, 2, 2)]
+STEPS_A = [("a", 0, 0), ("a", 0, 1), ("a", 0, 2), ("a", 0, 3), ("x", 0, 0), ("x", 0, 1), ("a", 1, 0), ("a", 1, 1), ("x", 0, 2), ("x", 0, 3), ("a", 1, 2), ("a", 1, 3), ("a", 2, 0), ("a", 2, 1), ("a", 2, 2), ("a", 2, 3)]
 SCALED_BUFS = 4
-AHEAD = 2
+HEAD_AHEAD = 2
+HEAD_STEPS = 8
+READY_AHEAD = 3
 SETUP_AT = 5
-SLACK = 2
+FINISH = "SVT"
+WARM = range(0, 8)
+SLACK = 3
 PART = 2
 BUDGET_A = 4
 BUDGET_B = 6
@@ -63,7 +64,7 @@ def tile_deepseekv3attention_pa_kernel(
         h_pool = ctx.enter_context(tc.tile_pool(name="h_pool", bufs=3))
         q_pool = ctx.enter_context(tc.tile_pool(name="q_pool", bufs=3))
         rope_pool = ctx.enter_context(tc.tile_pool(name="rope_pool", bufs=1))
-        out_pool = ctx.enter_context(tc.tile_pool(name="out_pool", bufs=2))
+        out_pool = ctx.enter_context(tc.tile_pool(name="out_pool", bufs=4))
         bank_pool = ctx.enter_context(tc.psum_pool(name="bank_pool", bufs=8 - ACCS))
         acc_pool = ctx.enter_context(tc.psum_pool(name="acc_pool", bufs=ACCS))
         ctx.enter_context(tc.manual_schedule())
@@ -176,8 +177,16 @@ def tile_deepseekv3attention_pa_kernel(
                 if kind == "b" and g == PASSES_B - 1 and n + RAW_BUFS[PASSES_B] < GROUPS_B:
                     load("b", n + RAW_BUFS[PASSES_B], 0, PASSES_B)
 
-        def transpose_pair(rows):
+        def transpose_pair(rows, keep_warm):
             bank = bank_pool.tile([P, 2, 2 * P], F32, name="bank", tag="bank")
+            if keep_warm:
+                nc.tensor.matmul(
+                    out=bank[:].rearrange("p u r -> p (u r)"),
+                    lhsT=ones[:],
+                    rhs=select[:].rearrange("p n i -> p (n i)")[:, 0:GROUP],
+                    start=True,
+                    stop=True,
+                )
             for u in range(2):
                 for x in range(2):
                     nc.tensor.transpose(
@@ -211,12 +220,12 @@ def tile_deepseekv3attention_pa_kernel(
             kind, n, g = item
             if kind == "h":
                 banks[item] = [
-                    transpose_pair([h_rows[2 * n + x][:, K_PASS * c : K_PASS * (c + 1)] for x in range(2)])
+                    transpose_pair([h_rows[2 * n + x][:, K_PASS * c : K_PASS * (c + 1)] for x in range(2)], place[item] in WARM)
                     for c in range(PASSES_B)
                 ]
             else:
                 banks[item] = [
-                    transpose_pair([raw[item][:, 2 * pair + x, :] for x in range(2)]) for pair in range(ROWS // 2)
+                    transpose_pair([raw[item][:, 2 * pair + x, :] for x in range(2)], place[item] in WARM) for pair in range(ROWS // 2)
                 ]
 
         def copies_out(item):
@@ -258,10 +267,20 @@ def tile_deepseekv3attention_pa_kernel(
         def in_order(columns):
             return columns.rearrange("t (r p) -> t p r", r=ROWS)
 
-        def finish_latent(c, b):
+        def sum_squares(c, b):
             acc = accs[("a", c, b)]
             squares = rope_pool.tile([P, GROUP], BF16, name="squares", tag="squares")
             nc.scalar.activation(out=squares[:], in_=acc[:], func=ACT.Square, accum_out=sum_sq[:, b, c : c + 1])
+            nc.scalar.activation(
+                out=mean_sq[:, b, c : c + 1],
+                in_=sum_sq[:, b, c : c + 1],
+                func=ACT.Sqrt if c == GROUPS_A - 1 else ACT.Identity,
+                scale=1.0 / LATENT,
+                bias=eps[:] if c == 0 else mean_sq[:, b, c - 1 : c],
+            )
+
+        def keep_latent(c, b):
+            acc = accs[("a", c, b)]
             cols = slice(GROUP * c, GROUP * (c + 1))
             if b == 0:
                 latents[c] = q_pool.tile([P, TOKEN_BLOCKS, GROUP], F32, name="q_sb", tag="q_sb")
@@ -271,19 +290,21 @@ def tile_deepseekv3attention_pa_kernel(
                 in1=gain[:, cols].rearrange("t (p r) -> t p r", r=ROWS),
                 op=ALU.mult,
             )
-            nc.scalar.activation(
-                out=mean_sq[:, b, c : c + 1],
-                in_=sum_sq[:, b, c : c + 1],
-                func=ACT.Sqrt if c == GROUPS_A - 1 else ACT.Identity,
-                scale=1.0 / LATENT,
-                bias=eps[:] if c == 0 else mean_sq[:, b, c - 1 : c],
-            )
 
         def normalise(b):
             one = slice(b, b + 1)
             nc.vector.reciprocal(out=inv_rms[:, one], in_=mean_sq[:, b, GROUPS_A - 1 : GROUPS_A])
             h_rows[b] = h_pool.tile([P, LATENT], BF16, name="h_row", tag="h_row")
-            for c in range(GROUPS_A):
+            last = slice(GROUP * (GROUPS_A - 1), LATENT)
+            nc.vector.scalar_tensor_tensor(
+                out=h_rows[b][:, last].rearrange("t (p r) -> t p r", r=ROWS),
+                in0=in_order(accs[("a", GROUPS_A - 1, b)][:]),
+                scalar=inv_rms[:, one],
+                in1=gain[:, last].rearrange("t (p r) -> t p r", r=ROWS),
+                op0=ALU.mult,
+                op1=ALU.mult,
+            )
+            for c in range(GROUPS_A - 1):
                 nc.vector.tensor_scalar_mul(
                     out=h_rows[b][:, GROUP * c : GROUP * (c + 1)], in0=latents[c][:, b, :], scalar1=inv_rms[:, one]
                 )
@@ -291,84 +312,75 @@ def tile_deepseekv3attention_pa_kernel(
         nope_out = out_0.rearrange("(b p) h x -> p b (h x)", p=P)
         rope_out = out_1.rearrange("(b p) h j -> p b (h j)", p=P)
         nope_tiles = {}
-        rope_tiles = {}
         partial = {}
 
         def unrotated_before(unit):
             return unit - unit // 3
 
         def rotated_before(unit):
-            return (unit + 0) // 3
-
-        def first_group(n):
-            return [s for s in SETS if n in s][0][0]
+            return unit // 3
 
         def part_of(n):
             return 1 if n == GROUPS_B - 1 else PART
 
-        def finish_query(n, b):
-            unit_0 = UNITS * first_group(n)
-            if b == 0 and n == first_group(n):
-                nope_tiles[n] = q_pool.tile([P, TOKEN_BLOCKS, SET_UNITS, ROPE], F32, name="q_sb", tag="q_sb")
-                rope_tiles[n] = out_pool.tile([P, TOKEN_BLOCKS, SET_HEADS, ROPE], F32, name="rotated", tag="rotated")
+        def units_of(n, b, kind):
+            first = (kind - UNITS * n) % 3
             by_unit = accs[("b", n, b)][:].rearrange("t (r s q) -> t s q r", r=ROWS, s=UNITS)
-            nope = nope_tiles[first_group(n)]
-            for kind in range(3):
-                first = (kind - UNITS * n) % 3
-                columns = by_unit[:, first:UNITS:3, :, :]
-                count = columns.shape[1]
-                if kind < 2:
-                    at = unrotated_before(UNITS * n + first) - unrotated_before(unit_0)
-                    nc.scalar.copy(
-                        out=nope[:, b, at : at + 2 * count - 1 : 2, :].rearrange("t s (q r) -> t s q r", r=ROWS),
-                        in_=columns,
-                    )
-                else:
-                    part = part_of(n)
-                    if b % part == 0:
-                        partial[(n, b // part_of(n))] = [
-                            rope_pool.tile([P, part, count, ROPE], F32, name=name, tag=name, bufs=2)
-                            for name in ("straight", "crossed")
-                        ]
-                    for product, table in zip(partial[(n, b // part_of(n))], (cos_sb, sin_swapped)):
-                        nc.vector.tensor_tensor(
-                            out=product[:, b % part, :, :].rearrange("t s (q r) -> t s q r", r=ROWS),
-                            in0=columns,
-                            in1=table[:, b, :]
-                            .rearrange("t (q r) -> t q r", r=ROWS)
-                            .unsqueeze(1)
-                            .to_broadcast([P, count, ROPE // ROWS, ROWS]),
-                            op=ALU.mult,
-                        )
+            return first, by_unit[:, first:UNITS:3, :, :]
+
+        def keep_unrotated(n, b):
+            if b == 0:
+                width = unrotated_before(UNITS * (n + 1)) - unrotated_before(UNITS * n)
+                nope_tiles[n] = q_pool.tile([P, TOKEN_BLOCKS, width, ROPE], F32, name="q_sb", tag="q_sb")
+            for kind in range(2):
+                first, columns = units_of(n, b, kind)
+                at = unrotated_before(UNITS * n + first) - unrotated_before(UNITS * n)
+                nc.scalar.copy(
+                    out=nope_tiles[n][:, b, at : at + 2 * columns.shape[1] - 1 : 2, :].rearrange(
+                        "t s (q r) -> t s q r", r=ROWS
+                    ),
+                    in_=columns,
+                )
+
+        def multiply_rotated(n, b):
+            part = part_of(n)
+            first, columns = units_of(n, b, 2)
+            count = columns.shape[1]
+            if b % part == 0:
+                partial[(n, b // part)] = [
+                    rope_pool.tile([P, part, count, ROPE], F32, name=name, tag=name, bufs=2)
+                    for name in ("straight", "crossed")
+                ]
+            for product, table in zip(partial[(n, b // part)], (cos_sb, sin_swapped)):
+                nc.vector.tensor_tensor(
+                    out=product[:, b % part, :, :].rearrange("t s (q r) -> t s q r", r=ROWS),
+                    in0=columns,
+                    in1=table[:, b, :]
+                    .rearrange("t (q r) -> t q r", r=ROWS)
+                    .unsqueeze(1)
+                    .to_broadcast([P, count, ROPE // ROWS, ROWS]),
+                    op=ALU.mult,
+                )
 
         def store_query(n, b):
-            unit_0 = UNITS * first_group(n)
-            nope = nope_tiles[first_group(n)]
             part = part_of(n)
+            if (b + 1) % part > 0:
+                return
             blocks = slice(b + 1 - part, b + 1)
-            if (b + 1) % part == 0:
-                straight, crossed = partial[(n, b // part_of(n))]
-                at = rotated_before(UNITS * n) - rotated_before(unit_0)
-                heads = slice(at, at + straight.shape[2])
-                rotated = rope_tiles[first_group(n)]
-                for half, other in ((low, high), (high, low)):
-                    nc.vector.tensor_tensor(
-                        out=rotated[:, blocks, heads, half],
-                        in0=straight[:, :, :, half],
-                        in1=crossed[:, :, :, other],
-                        op=ALU.add,
-                    )
-                if n == [s for s in SETS if n in s][0][-1]:
-                    end = UNITS * (n + 1)
-                    for out, tile, before in (
-                        (nope_out, nope, unrotated_before),
-                        (rope_out, rotated, rotated_before),
-                    ):
-                        width = before(end) - before(unit_0)
-                        nc.sync.dma_start(
-                            out=out[:, blocks, ROPE * before(unit_0) : ROPE * before(end)],
-                            in_=tile[:, blocks, 0:width, :].rearrange("p b s j -> p b (s j)"),
-                        )
+            nc.sync.dma_start(
+                out=nope_out[:, blocks, ROPE * unrotated_before(UNITS * n) : ROPE * unrotated_before(UNITS * (n + 1))],
+                in_=nope_tiles[n][:, blocks, :, :].rearrange("p b s j -> p b (s j)"),
+            )
+            straight, crossed = partial[(n, b // part)]
+            rotated = out_pool.tile(list(straight.shape), F32, name="rotated", tag="rotated")
+            for half, other in ((low, high), (high, low)):
+                nc.vector.tensor_tensor(
+                    out=rotated[:, :, :, half], in0=straight[:, :, :, half], in1=crossed[:, :, :, other], op=ALU.add
+                )
+            nc.sync.dma_start(
+                out=rope_out[:, blocks, ROPE * rotated_before(UNITS * n) : ROPE * rotated_before(UNITS * (n + 1))],
+                in_=rotated[:].rearrange("p b s j -> p b (s j)"),
+            )
 
         a_items = []
         singles = STEPS_A
@@ -396,9 +408,11 @@ def tile_deepseekv3attention_pa_kernel(
             act = ("x", 0, g) if kind == "a" else ("h", b // 2, 0)
             return max(place[(kind, n, g)], place[act])
 
-        for i in range(AHEAD):
+        scaled_steps = 0
+        for i in range(HEAD_AHEAD):
             for item in steps[i]:
                 prescale(item)
+            scaled_steps += 1
         closed = []
         live = 0
         done = 0
@@ -406,22 +420,26 @@ def tile_deepseekv3attention_pa_kernel(
         while done < len(products) or len(closed) > 0:
             if i == SETUP_AT:
                 setup()
-            for kind, n, b in closed:
-                if kind == "a":
-                    finish_latent(n, b)
-                else:
-                    finish_query(n, b)
-            if i < len(steps):
-                for item in steps[i]:
-                    transposes(item)
-                for item in steps[i]:
-                    copies_out(item)
+            for what in FINISH:
+                if what == "T" and i < len(steps):
+                    for item in steps[i]:
+                        transposes(item)
+                    for item in steps[i]:
+                        copies_out(item)
+                if what == "V":
+                    for kind, n, b in closed:
+                        if (kind, n) != ("a", GROUPS_A - 1):
+                            (keep_latent if kind == "a" else multiply_rotated)(n, b)
+                if what == "S":
+                    for kind, n, b in closed:
+                        (sum_squares if kind == "a" else keep_unrotated)(n, b)
             if 1 <= i <= len(steps):
                 for item in steps[i - 1]:
                     quantises(item)
-            if i + AHEAD < len(steps):
-                for item in steps[i + AHEAD]:
+            while scaled_steps < len(steps) and scaled_steps <= i + (HEAD_AHEAD if i < HEAD_STEPS else READY_AHEAD):
+                for item in steps[scaled_steps]:
                     prescale(item)
+                scaled_steps += 1
             for kind, n, b in closed:
                 if (kind, n) == ("a", GROUPS_A - 1):
                     normalise(b)

@@ -37,12 +37,11 @@ H_AT = (6, 7)
 LOADS = [("a", 0, 0, 1), ("a", 0, 1, 1), ("a", 0, 2, 2), (), ("x", 0, 0, 2), ("a", 1, 0, 2), ("x", 0, 2, 2), ("a", 1, 2, 2), ("a", 2, 0, 2), ("a", 2, 2, 2)]
 STEPS_A = [("a", 0, 0), ("a", 0, 1), ("a", 0, 2), ("a", 0, 3), ("x", 0, 0), ("x", 0, 1), ("a", 1, 0), ("a", 1, 1), ("x", 0, 2), ("x", 0, 3), ("a", 1, 2), ("a", 1, 3), ("a", 2, 0), ("a", 2, 1), ("a", 2, 2), ("a", 2, 3)]
 SCALED_BUFS = 4
-HEAD_AHEAD = 2
-HEAD_STEPS = 8
-READY_AHEAD = 3
-SETUP_AT = 5
+AHEAD = 3
+SETUP_AT = 4
 FINISH = "SVT"
-WARM = range(0, 8)
+WARM = list(range(0, 8)) + list(range(22, 25))
+TAIL = "NSP"
 SLACK = 3
 PART = 2
 BUDGET_A = 4
@@ -409,7 +408,7 @@ def tile_deepseekv3attention_pa_kernel(
             return max(place[(kind, n, g)], place[act])
 
         scaled_steps = 0
-        for i in range(HEAD_AHEAD):
+        for i in range(AHEAD):
             for item in steps[i]:
                 prescale(item)
             scaled_steps += 1
@@ -436,15 +435,17 @@ def tile_deepseekv3attention_pa_kernel(
             if 1 <= i <= len(steps):
                 for item in steps[i - 1]:
                     quantises(item)
-            while scaled_steps < len(steps) and scaled_steps <= i + (HEAD_AHEAD if i < HEAD_STEPS else READY_AHEAD):
-                for item in steps[scaled_steps]:
-                    prescale(item)
-                scaled_steps += 1
-            for kind, n, b in closed:
-                if (kind, n) == ("a", GROUPS_A - 1):
-                    normalise(b)
-                if kind == "b":
-                    store_query(n, b)
+            for what in TAIL:
+                if what == "P":
+                    while scaled_steps < len(steps) and scaled_steps <= i + AHEAD:
+                        for item in steps[scaled_steps]:
+                            prescale(item)
+                        scaled_steps += 1
+                for kind, n, b in closed:
+                    if what == "N" and (kind, n) == ("a", GROUPS_A - 1):
+                        normalise(b)
+                    if what == "S" and kind == "b":
+                        store_query(n, b)
             live -= len(closed)
             closed = []
             budget = BUDGET_A if i < place[("h", 0, 0)] else BUDGET_B

@@ -40,7 +40,6 @@ SCALED_BUFS = 4
 AHEAD = 3
 SETUP_AT = 4
 FINISH = "SVT"
-WARM = list(range(0, 8)) + list(range(22, 25))
 TAIL = "NSP"
 SLACK = 3
 PART = 2
@@ -176,16 +175,8 @@ def tile_deepseekv3attention_pa_kernel(
                 if kind == "b" and g == PASSES_B - 1 and n + RAW_BUFS[PASSES_B] < GROUPS_B:
                     load("b", n + RAW_BUFS[PASSES_B], 0, PASSES_B)
 
-        def transpose_pair(rows, keep_warm):
+        def transpose_pair(rows):
             bank = bank_pool.tile([P, 2, 2 * P], F32, name="bank", tag="bank")
-            if keep_warm:
-                nc.tensor.matmul(
-                    out=bank[:].rearrange("p u r -> p (u r)"),
-                    lhsT=ones[:],
-                    rhs=select[:].rearrange("p n i -> p (n i)")[:, 0:GROUP],
-                    start=True,
-                    stop=True,
-                )
             for u in range(2):
                 for x in range(2):
                     nc.tensor.transpose(
@@ -219,12 +210,12 @@ def tile_deepseekv3attention_pa_kernel(
             kind, n, g = item
             if kind == "h":
                 banks[item] = [
-                    transpose_pair([h_rows[2 * n + x][:, K_PASS * c : K_PASS * (c + 1)] for x in range(2)], place[item] in WARM)
+                    transpose_pair([h_rows[2 * n + x][:, K_PASS * c : K_PASS * (c + 1)] for x in range(2)])
                     for c in range(PASSES_B)
                 ]
             else:
                 banks[item] = [
-                    transpose_pair([raw[item][:, 2 * pair + x, :] for x in range(2)], place[item] in WARM) for pair in range(ROWS // 2)
+                    transpose_pair([raw[item][:, 2 * pair + x, :] for x in range(2)]) for pair in range(ROWS // 2)
                 ]
 
         def copies_out(item):

@@ -29,24 +29,15 @@ PASSES_B = LATENT // K_PASS
 GROUPS_A = LATENT // GROUP
 GROUPS_B = HEADS * HEAD // GROUP
 TOKEN_BLOCKS = TOKENS // P
+UNITS = GROUP // ROPE
 FLOPS = 2 * TOKENS * HIDDEN * LATENT + 2 * TOKENS * LATENT * HEADS * HEAD
 
-RAW_BUFS = {1: 2, 2: 5, 3: 3}
-UNITS = GROUP // ROPE
-H_AT = (6, 7)
-LOADS = [("a", 0, 0, 1), ("a", 0, 1, 1), ("a", 0, 2, 2), (), ("x", 0, 0, 2), ("a", 1, 0, 2), ("x", 0, 2, 2), ("a", 1, 2, 2), ("a", 2, 0, 2), ("a", 2, 2, 2)]
-STEPS_A = [("a", 0, 0), ("a", 0, 1), ("a", 0, 2), ("a", 0, 3), ("x", 0, 0), ("x", 0, 1), ("a", 1, 0), ("a", 1, 1), ("x", 0, 2), ("x", 0, 3), ("a", 1, 2), ("a", 1, 3), ("a", 2, 0), ("a", 2, 1), ("a", 2, 2), ("a", 2, 3)]
-SCALED_BUFS = 4
-AHEAD = 3
-SETUP_AT = 4
-FINISH = "SVT"
-TAIL = "NSP"
-SLACK = 3
-PART = 2
-BUDGET_A = 4
-BUDGET_B = 6
-TOGETHER = 1
-ACCS = 4
+LOADS_A = (("a", 0, 0), ("a", 0, 1), ("x", 0, 0), ("a", 1, 0), ("x", 0, 1), ("a", 1, 1), ("a", 2, 0), ("a", 2, 1))
+AHEAD_OF_H = (6, 7)
+SCALE_AHEAD = 3
+MULTIPLY_BEHIND = 3
+SETUP_STEP = 4
+SUM_BANKS = 4
 
 
 def tile_deepseekv3attention_pa_kernel(
@@ -55,54 +46,57 @@ def tile_deepseekv3attention_pa_kernel(
     nc = tc.nc
     with ExitStack() as ctx:
         keep = ctx.enter_context(tc.tile_pool(name="keep", bufs=1))
-        raw_pool = ctx.enter_context(tc.tile_pool(name="raw_pool", bufs=1))
-        scaled_pool = ctx.enter_context(tc.tile_pool(name="scaled_pool", bufs=SCALED_BUFS))
+        half_pool = ctx.enter_context(tc.tile_pool(name="half_pool", bufs=5))
+        group_pool = ctx.enter_context(tc.tile_pool(name="group_pool", bufs=3))
+        scaled_pool = ctx.enter_context(tc.tile_pool(name="scaled_pool", bufs=SCALE_AHEAD + 1))
         grouped_pool = ctx.enter_context(tc.tile_pool(name="grouped_pool", bufs=4))
         weight_pool = ctx.enter_context(tc.tile_pool(name="weight_pool", bufs=14))
         h_pool = ctx.enter_context(tc.tile_pool(name="h_pool", bufs=3))
         q_pool = ctx.enter_context(tc.tile_pool(name="q_pool", bufs=3))
-        rope_pool = ctx.enter_context(tc.tile_pool(name="rope_pool", bufs=1))
-        out_pool = ctx.enter_context(tc.tile_pool(name="out_pool", bufs=4))
-        bank_pool = ctx.enter_context(tc.psum_pool(name="bank_pool", bufs=8 - ACCS))
-        acc_pool = ctx.enter_context(tc.psum_pool(name="acc_pool", bufs=ACCS))
+        squares_pool = ctx.enter_context(tc.tile_pool(name="squares_pool", bufs=1))
+        product_pool = ctx.enter_context(tc.tile_pool(name="product_pool", bufs=2))
+        rotated_pool = ctx.enter_context(tc.tile_pool(name="rotated_pool", bufs=4))
+        bank_pool = ctx.enter_context(tc.psum_pool(name="bank_pool", bufs=8 - SUM_BANKS))
+        sum_pool = ctx.enter_context(tc.psum_pool(name="sum_pool", bufs=SUM_BANKS))
         ctx.enter_context(tc.manual_schedule())
 
-        sq_rows = keep.tile([P, sq_a.shape[1] + sq_b.shape[1]], BF16)
+        n_k_a = sq_a.shape[1]
+        n_k_b = sq_b.shape[1]
+        sq_rows = keep.tile([P, n_k_a + n_k_b], BF16)
         nc.vector.memset(sq_rows[:], 0.0)
-        nc.sync.dma_start(out=sq_rows[0 : sq_a.shape[0], 0 : sq_a.shape[1]], in_=sq_a)
-        nc.sync.dma_start(out=sq_rows[0 : sq_b.shape[0], sq_a.shape[1] :], in_=sq_b)
+        nc.sync.dma_start(out=sq_rows[0 : sq_a.shape[0], 0:n_k_a], in_=sq_a)
+        nc.sync.dma_start(out=sq_rows[0 : sq_b.shape[0], n_k_a:], in_=sq_b)
         gain_row = h_pool.tile([P, LATENT], BF16, name="h_row", tag="h_row")
         nc.vector.memset(gain_row[:], 0.0)
         cos_bf = keep.tile([P, TOKEN_BLOCKS, ROPE], BF16)
         sin_bf = keep.tile([P, TOKEN_BLOCKS, ROPE], BF16)
-
-        def load_small():
-            nc.sync.dma_start(out=gain_row[0:1, :], in_=q_ln_w.unsqueeze(0))
-            nc.sync.dma_start(out=cos_bf[:], in_=cos.rearrange("(b p) j -> p b j", p=P))
-            nc.sync.dma_start(out=sin_bf[:], in_=sin.rearrange("(b p) j -> p b j", p=P))
-
         raw = {}
 
-        def load(kind, n, first, count):
-            tag = "raw_%d" % count
-            tile = raw_pool.tile([P, ROWS, K_PASS * count], BF16, name=tag, tag=tag, bufs=RAW_BUFS[count])
-            cols = slice(K_PASS * first, K_PASS * (first + count))
+        def operand_rows(kind, n):
             if kind == "x":
-                rows = hidden_states.rearrange("(b p) k -> p b k", p=P)
-            else:
-                weights = wq_a if kind == "a" else wq_b
-                rows = weights[GROUP * n : GROUP * (n + 1), :].rearrange("(p r) k -> p r k", r=ROWS)
-            nc.sync.dma_start(out=tile[:], in_=rows[:, :, cols])
-            for g in range(count):
-                raw[(kind, n, first + g)] = tile[:, :, K_PASS * g : K_PASS * (g + 1)]
+                return hidden_states.rearrange("(b p) k -> p b k", p=P)
+            weights = wq_a if kind == "a" else wq_b
+            return weights[GROUP * n : GROUP * (n + 1), :].rearrange("(p r) k -> p r k", r=ROWS)
 
-        for args in LOADS:
-            if args:
-                load(*args)
-            else:
-                load_small()
-        for n in range(RAW_BUFS[PASSES_B]):
-            load("b", n, 0, PASSES_B)
+        def load_half(kind, n, half):
+            tile = half_pool.tile([P, 2, HIDDEN], BF16, name="raw_half", tag="raw_half")
+            nc.sync.dma_start(out=tile[:], in_=operand_rows(kind, n)[:, 2 * half : 2 * half + 2, :])
+            raw[(kind, n, half)] = tile
+
+        def load_group(n):
+            tile = group_pool.tile([P, ROWS, LATENT], BF16, name="raw_group", tag="raw_group")
+            nc.sync.dma_start(out=tile[:], in_=operand_rows("b", n))
+            raw[("b", n, 0)] = tile
+
+        for j in range(len(LOADS_A)):
+            load_half(*LOADS_A[j])
+            if j == 1:
+                nc.sync.dma_start(out=gain_row[0:1, :], in_=q_ln_w.unsqueeze(0))
+        nc.sync.dma_start(out=cos_bf[:], in_=cos.rearrange("(b p) j -> p b j", p=P))
+        nc.sync.dma_start(out=sin_bf[:], in_=sin.rearrange("(b p) j -> p b j", p=P))
+        groups_loaded = 3
+        for n in range(groups_loaded):
+            load_group(n)
 
         ident = keep.tile([P, P], F32)
         masks.make_identity(nc, ident[:])
@@ -110,12 +104,12 @@ def tile_deepseekv3attention_pa_kernel(
         nc.vector.memset(ones[:], 1.0)
         eps = keep.tile([P, 1], F32)
         nc.vector.memset(eps[:], EPS)
-        warm = keep.tile([P, 1], F32)
-        nc.scalar.activation(out=warm[:], in_=eps[:], func=ACT.Sqrt)
+        first_sqrt = keep.tile([P, 1], F32)
+        nc.scalar.activation(out=first_sqrt[:], in_=eps[:], func=ACT.Sqrt)
 
         select = keep.tile([P, GROUPS_B, P], BF16)
         nc.vector.tensor_copy(
-            out=select[:].rearrange("p n (q i) -> p (n q) i", i=32),
+            out=select[:].rearrange("b n (q i) -> b (n q) i", i=32),
             in_=ident[:, 0 : 4 * GROUPS_B].unsqueeze(2).to_broadcast([P, 4 * GROUPS_B, 32]),
         )
         factors = {}
@@ -133,59 +127,84 @@ def tile_deepseekv3attention_pa_kernel(
             factors[kind] = keep.tile([P, groups, width], F32, name="factors_" + kind)
             nc.scalar.copy(out=factors[kind][:], in_=bank[:])
 
-        factor_table("a", GROUPS_A, 0, sq_a.shape[1])
-
+        factor_table("a", GROUPS_A, 0, n_k_a)
         gain = keep.tile([P, LATENT], F32)
-        half_rope = ROPE // 2
-        low = slice(0, half_rope)
-        high = slice(half_rope, ROPE)
-        cos_sb = keep.tile([P, TOKEN_BLOCKS, ROPE], F32)
-        nc.gpsimd.tensor_copy(out=cos_sb[:], in_=cos_bf[:])
-        sin_swapped = keep.tile([P, TOKEN_BLOCKS, ROPE], F32)
-        nc.gpsimd.tensor_copy(out=sin_swapped[:, :, low], in_=sin_bf[:, :, high])
-        nc.gpsimd.tensor_scalar(
-            out=sin_swapped[:, :, high], in0=sin_bf[:, :, low], scalar1=-1.0, scalar2=0.0, op0=ALU.mult, op1=ALU.add
-        )
 
         def setup():
-            factor_table("b", GROUPS_B, sq_a.shape[1], sq_b.shape[1])
-            for n in range(LATENT // GROUP):
+            factor_table("b", GROUPS_B, n_k_a, n_k_b)
+            for n in range(GROUPS_A):
                 cols = slice(GROUP * n, GROUP * (n + 1))
                 bank = bank_pool.tile([P, GROUP], F32, name="bank", tag="bank")
                 nc.tensor.matmul(out=bank[:], lhsT=ones[:], rhs=gain_row[:, cols], start=True, stop=True)
                 nc.scalar.copy(out=gain[:, cols], in_=bank[:])
 
+        low = slice(0, ROPE // 2)
+        high = slice(ROPE // 2, ROPE)
+        cos_sb = keep.tile([P, TOKEN_BLOCKS, ROPE], F32)
+        sin_swapped = keep.tile([P, TOKEN_BLOCKS, ROPE], F32)
+
+        def rotation_tables():
+            nc.vector.tensor_copy(out=cos_sb[:], in_=cos_bf[:])
+            nc.vector.tensor_copy(out=sin_swapped[:, :, low], in_=sin_bf[:, :, high])
+            nc.vector.tensor_scalar_mul(out=sin_swapped[:, :, high], in0=sin_bf[:, :, low], scalar1=-1.0)
+
+        item_rows = {}
         banks = {}
         grouped = {}
         codes = {}
         scales = {}
+        x_codes = keep.tile([P, PASSES_A, TOKENS], U32, align_bytes=64)
+        x_scales = keep.tile([P, PASSES_A, TOKENS], U8, align_bytes=64)
+        h_codes = keep.tile([P, PASSES_B, TOKENS], U32, align_bytes=64)
+        h_scales = keep.tile([P, PASSES_B, TOKENS], U8, align_bytes=64)
+        h_rows = {}
 
-        def prescale(item):
-            kind, n, g = item
-            if kind in factors:
-                scaled = scaled_pool.tile([P, ROWS, K_PASS], BF16, name="scaled", tag="scaled")
-                for c in range(ROWS):
-                    cols = slice(P * c, P * (c + 1))
-                    nc.vector.tensor_scalar_mul(
-                        out=scaled[:, :, cols],
-                        in0=raw[item][:, :, cols],
-                        scalar1=factors[kind][:, n, 4 * g + c : 4 * g + c + 1],
-                    )
-                raw[item] = scaled
-                if kind == "b" and g == PASSES_B - 1 and n + RAW_BUFS[PASSES_B] < GROUPS_B:
-                    load("b", n + RAW_BUFS[PASSES_B], 0, PASSES_B)
+        def scale(item):
+            kind, n, half, passes = item
+            if kind == "h":
+                return
+            source = raw[(kind, n, half)]
+            first = K_PASS * passes[0]
+            width = K_PASS * len(passes)
+            if kind == "x":
+                item_rows[item] = source[:, :, first : first + width]
+                return
+            scaled = scaled_pool.tile([P, source.shape[1], width], BF16, name="scaled", tag="scaled")
+            for c in range(width // P):
+                k_block = first // P + c
+                nc.vector.tensor_scalar_mul(
+                    out=scaled[:, :, P * c : P * (c + 1)],
+                    in0=source[:, :, P * k_block : P * (k_block + 1)],
+                    scalar1=factors[kind][:, n, k_block : k_block + 1],
+                )
+            item_rows[item] = scaled
+            if kind == "b" and passes[-1] == PASSES_B - 1 and n + groups_loaded < GROUPS_B:
+                load_group(n + groups_loaded)
 
         def transpose_pair(rows):
             bank = bank_pool.tile([P, 2, 2 * P], F32, name="bank", tag="bank")
             for u in range(2):
                 for x in range(2):
-                    nc.tensor.transpose(
-                        bank[:, u, P * x : P * (x + 1)], rows[x].bitcast(F32)[:, P * u : P * (u + 1)], ident[:]
-                    )
+                    words = rows[x].bitcast(F32)[:, P * u : P * (u + 1)]
+                    nc.tensor.transpose(bank[:, u, P * x : P * (x + 1)], words, ident[:])
             return bank
 
+        def transpose(item):
+            kind, n, half, passes = item
+            banks[item] = []
+            for i in range(len(passes)):
+                cols = slice(K_PASS * i, K_PASS * (i + 1))
+                if kind == "h":
+                    banks[item].append(transpose_pair([h_rows[2 * half + x][:, cols] for x in range(2)]))
+                else:
+                    rows = item_rows[item]
+                    for pair in range(rows.shape[1] // 2):
+                        banks[item].append(transpose_pair([rows[:, 2 * pair + x, cols] for x in range(2)]))
+
         def copy_out(some_banks):
-            tile = grouped_pool.tile([P, 2 * P * len(some_banks), 4], BF16, name="grouped", tag="grouped", align_bytes=64)
+            tile = grouped_pool.tile(
+                [P, 2 * P * len(some_banks), 4], BF16, name="grouped", tag="grouped", align_bytes=64
+            )
             for i in range(len(some_banks)):
                 nc.scalar.copy(
                     out=tile[:, 2 * P * i : 2 * P * (i + 1), :].bitcast(F32),
@@ -193,59 +212,49 @@ def tile_deepseekv3attention_pa_kernel(
                 )
             return tile
 
-        def quantise(tile, out, out_scales):
-            nc.vector.quantize_mx(out=out.bitcast(FP8X4), scales=out_scales, in_=tile[:].rearrange("p r t -> p (r t)"))
-
-        h_codes = keep.tile([P, PASSES_B, TOKENS], U32, align_bytes=64)
-        h_scales = keep.tile([P, PASSES_B, TOKENS], U8, align_bytes=64)
-        x_codes = keep.tile([P, PASSES_A, TOKENS], U32, align_bytes=64)
-        x_scales = keep.tile([P, PASSES_A, TOKENS], U8, align_bytes=64)
-        latents = {}
-        sum_sq = keep.tile([P, TOKEN_BLOCKS, GROUPS_A], F32)
-        mean_sq = keep.tile([P, TOKEN_BLOCKS, GROUPS_A], F32)
-        inv_rms = keep.tile([P, TOKEN_BLOCKS], F32)
-        h_rows = {}
-
-        def transposes(item):
-            kind, n, g = item
-            if kind == "h":
-                banks[item] = [
-                    transpose_pair([h_rows[2 * n + x][:, K_PASS * c : K_PASS * (c + 1)] for x in range(2)])
-                    for c in range(PASSES_B)
-                ]
-            else:
-                banks[item] = [
-                    transpose_pair([raw[item][:, 2 * pair + x, :] for x in range(2)]) for pair in range(ROWS // 2)
-                ]
-
-        def copies_out(item):
+        def empty(item):
             if item[0] == "h":
                 grouped[item] = [copy_out([bank]) for bank in banks[item]]
             else:
                 grouped[item] = [copy_out(banks[item])]
 
-        def quantises(item):
-            kind, n, g = item
-            if kind == "h":
-                cols = slice(2 * P * n, 2 * P * (n + 1))
-                for c in range(PASSES_B):
-                    quantise(grouped[item][c], h_codes[:, c, cols], h_scales[:, c, cols])
-            elif kind == "x":
-                quantise(grouped[item][0], x_codes[:, g, :], x_scales[:, g, :])
-            else:
-                codes[item] = weight_pool.tile([P, GROUP], U32, name="w_codes", tag="w_codes", align_bytes=64)
-                scales[item] = weight_pool.tile([P, GROUP], U8, name="w_scales", tag="w_scales", align_bytes=64)
-                quantise(grouped[item][0], codes[item][:], scales[item][:])
+        def quantise_rows(rows, out, out_scales):
+            nc.vector.quantize_mx(out=out.bitcast(FP8X4), scales=out_scales, in_=rows.rearrange("p r t -> p (r t)"))
 
-        accs = {}
+        def quantise(item):
+            kind, n, half, passes = item
+            cols = slice(2 * P * half, 2 * P * (half + 1))
+            if kind in "ab" and half == 0:
+                for g in passes:
+                    codes[(kind, n, g)] = weight_pool.tile(
+                        [P, GROUP], U32, name="w_codes", tag="w_codes", align_bytes=64
+                    )
+                    scales[(kind, n, g)] = weight_pool.tile(
+                        [P, GROUP], U8, name="w_scales", tag="w_scales", align_bytes=64
+                    )
+            if kind == "b":
+                quantise_rows(grouped[item][0][:], codes[(kind, n, passes[0])][:], scales[(kind, n, passes[0])][:])
+                return
+            for i in range(len(passes)):
+                g = passes[i]
+                if kind == "h":
+                    quantise_rows(grouped[item][i][:], h_codes[:, g, cols], h_scales[:, g, cols])
+                else:
+                    rows = grouped[item][0][:, 2 * P * i : 2 * P * (i + 1), :]
+                    if kind == "x":
+                        quantise_rows(rows, x_codes[:, g, cols], x_scales[:, g, cols])
+                    else:
+                        quantise_rows(rows, codes[(kind, n, g)][:, cols], scales[(kind, n, g)][:, cols])
+
+        sums = {}
 
         def multiply(kind, n, b, g, passes):
             if g == 0:
-                accs[(kind, n, b)] = acc_pool.tile([P, GROUP], F32, name="acc", tag="acc")
+                sums[(kind, n, b)] = sum_pool.tile([P, GROUP], F32, name="sum", tag="sum")
             act_codes, act_scales = (x_codes, x_scales) if kind == "a" else (h_codes, h_scales)
             tokens = slice(P * b, P * (b + 1))
             nc.tensor.matmul_mx(
-                out=accs[(kind, n, b)][:],
+                out=sums[(kind, n, b)][:],
                 lhsT=act_codes[:, g, tokens].bitcast(FP8X4),
                 lhsT_scale=act_scales[:, g, tokens],
                 rhs=codes[(kind, n, g)][:].bitcast(FP8X4),
@@ -254,30 +263,40 @@ def tile_deepseekv3attention_pa_kernel(
                 stop=(g == passes - 1),
             )
 
-        def in_order(columns):
+        latents = {}
+        sum_sq = keep.tile([P, TOKEN_BLOCKS, GROUPS_A], F32)
+        mean_sq = keep.tile([P, TOKEN_BLOCKS, GROUPS_A], F32)
+        inv_rms = keep.tile([P, TOKEN_BLOCKS], F32)
+
+        def in_row_order(columns):
             return columns.rearrange("t (r p) -> t p r", r=ROWS)
 
-        def sum_squares(c, b):
-            acc = accs[("a", c, b)]
-            squares = rope_pool.tile([P, GROUP], BF16, name="squares", tag="squares")
-            nc.scalar.activation(out=squares[:], in_=acc[:], func=ACT.Square, accum_out=sum_sq[:, b, c : c + 1])
+        def by_rows(columns):
+            return columns.rearrange("t (p r) -> t p r", r=ROWS)
+
+        def sum_squares(n, b):
+            squares = squares_pool.tile([P, GROUP], BF16, name="squares", tag="squares")
             nc.scalar.activation(
-                out=mean_sq[:, b, c : c + 1],
-                in_=sum_sq[:, b, c : c + 1],
-                func=ACT.Sqrt if c == GROUPS_A - 1 else ACT.Identity,
+                out=squares[:], in_=sums[("a", n, b)][:], func=ACT.Square, accum_out=sum_sq[:, b, n : n + 1]
+            )
+            nc.scalar.activation(
+                out=mean_sq[:, b, n : n + 1],
+                in_=sum_sq[:, b, n : n + 1],
+                func=ACT.Sqrt if n == GROUPS_A - 1 else ACT.Identity,
                 scale=1.0 / LATENT,
-                bias=eps[:] if c == 0 else mean_sq[:, b, c - 1 : c],
+                bias=eps[:] if n == 0 else mean_sq[:, b, n - 1 : n],
             )
 
-        def keep_latent(c, b):
-            acc = accs[("a", c, b)]
-            cols = slice(GROUP * c, GROUP * (c + 1))
+        def keep_latent(n, b):
+            if n == GROUPS_A - 1:
+                return
+            cols = slice(GROUP * n, GROUP * (n + 1))
             if b == 0:
-                latents[c] = q_pool.tile([P, TOKEN_BLOCKS, GROUP], F32, name="q_sb", tag="q_sb")
+                latents[n] = q_pool.tile([P, TOKEN_BLOCKS, GROUP], F32, name="q_sb", tag="q_sb")
             nc.vector.tensor_tensor(
-                out=latents[c][:, b, :].rearrange("t (p r) -> t p r", r=ROWS),
-                in0=in_order(acc[:]),
-                in1=gain[:, cols].rearrange("t (p r) -> t p r", r=ROWS),
+                out=by_rows(latents[n][:, b, :]),
+                in0=in_row_order(sums[("a", n, b)][:]),
+                in1=by_rows(gain[:, cols]),
                 op=ALU.mult,
             )
 
@@ -287,22 +306,22 @@ def tile_deepseekv3attention_pa_kernel(
             h_rows[b] = h_pool.tile([P, LATENT], BF16, name="h_row", tag="h_row")
             last = slice(GROUP * (GROUPS_A - 1), LATENT)
             nc.vector.scalar_tensor_tensor(
-                out=h_rows[b][:, last].rearrange("t (p r) -> t p r", r=ROWS),
-                in0=in_order(accs[("a", GROUPS_A - 1, b)][:]),
+                out=by_rows(h_rows[b][:, last]),
+                in0=in_row_order(sums[("a", GROUPS_A - 1, b)][:]),
                 scalar=inv_rms[:, one],
-                in1=gain[:, last].rearrange("t (p r) -> t p r", r=ROWS),
+                in1=by_rows(gain[:, last]),
                 op0=ALU.mult,
                 op1=ALU.mult,
             )
-            for c in range(GROUPS_A - 1):
+            for n in range(GROUPS_A - 1):
                 nc.vector.tensor_scalar_mul(
-                    out=h_rows[b][:, GROUP * c : GROUP * (c + 1)], in0=latents[c][:, b, :], scalar1=inv_rms[:, one]
+                    out=h_rows[b][:, GROUP * n : GROUP * (n + 1)], in0=latents[n][:, b, :], scalar1=inv_rms[:, one]
                 )
 
         nope_out = out_0.rearrange("(b p) h x -> p b (h x)", p=P)
         rope_out = out_1.rearrange("(b p) h j -> p b (h j)", p=P)
-        nope_tiles = {}
-        partial = {}
+        unrotated = {}
+        products = {}
 
         def unrotated_before(unit):
             return unit - unit // 3
@@ -310,146 +329,129 @@ def tile_deepseekv3attention_pa_kernel(
         def rotated_before(unit):
             return unit // 3
 
-        def part_of(n):
-            return 1 if n == GROUPS_B - 1 else PART
+        def blocks_together(n):
+            return 1 if n == GROUPS_B - 1 else 2
 
-        def units_of(n, b, kind):
-            first = (kind - UNITS * n) % 3
-            by_unit = accs[("b", n, b)][:].rearrange("t (r s q) -> t s q r", r=ROWS, s=UNITS)
-            return first, by_unit[:, first:UNITS:3, :, :]
+        def units_of(n, b, remainder):
+            first = (remainder - UNITS * n) % 3
+            by_unit = sums[("b", n, b)][:].rearrange("t (r u q) -> t u q r", r=ROWS, u=UNITS)
+            return by_unit[:, first:UNITS:3, :, :], first
 
-        def keep_unrotated(n, b):
+        def copy_unrotated(n, b):
+            unit_0 = UNITS * n
             if b == 0:
-                width = unrotated_before(UNITS * (n + 1)) - unrotated_before(UNITS * n)
-                nope_tiles[n] = q_pool.tile([P, TOKEN_BLOCKS, width, ROPE], F32, name="q_sb", tag="q_sb")
-            for kind in range(2):
-                first, columns = units_of(n, b, kind)
-                at = unrotated_before(UNITS * n + first) - unrotated_before(UNITS * n)
-                nc.scalar.copy(
-                    out=nope_tiles[n][:, b, at : at + 2 * columns.shape[1] - 1 : 2, :].rearrange(
-                        "t s (q r) -> t s q r", r=ROWS
-                    ),
-                    in_=columns,
-                )
+                width = unrotated_before(unit_0 + UNITS) - unrotated_before(unit_0)
+                unrotated[n] = q_pool.tile([P, TOKEN_BLOCKS, width, ROPE], F32, name="q_sb", tag="q_sb")
+            for remainder in range(2):
+                columns, first = units_of(n, b, remainder)
+                at = unrotated_before(unit_0 + first) - unrotated_before(unit_0)
+                places = unrotated[n][:, b, at : at + 2 * columns.shape[1] - 1 : 2, :]
+                nc.scalar.copy(out=places.rearrange("t u (q r) -> t u q r", r=ROWS), in_=columns)
 
         def multiply_rotated(n, b):
-            part = part_of(n)
-            first, columns = units_of(n, b, 2)
+            together = blocks_together(n)
+            columns, first = units_of(n, b, 2)
             count = columns.shape[1]
-            if b % part == 0:
-                partial[(n, b // part)] = [
-                    rope_pool.tile([P, part, count, ROPE], F32, name=name, tag=name, bufs=2)
+            if b % together == 0:
+                products[n] = [
+                    product_pool.tile([P, together, count, ROPE], F32, name=name, tag=name)
                     for name in ("straight", "crossed")
                 ]
-            for product, table in zip(partial[(n, b // part)], (cos_sb, sin_swapped)):
+            for product, table in zip(products[n], (cos_sb, sin_swapped)):
+                factor = table[:, b, :].rearrange("t (q r) -> t q r", r=ROWS).unsqueeze(1)
                 nc.vector.tensor_tensor(
-                    out=product[:, b % part, :, :].rearrange("t s (q r) -> t s q r", r=ROWS),
+                    out=product[:, b % together, :, :].rearrange("t u (q r) -> t u q r", r=ROWS),
                     in0=columns,
-                    in1=table[:, b, :]
-                    .rearrange("t (q r) -> t q r", r=ROWS)
-                    .unsqueeze(1)
-                    .to_broadcast([P, count, ROPE // ROWS, ROWS]),
+                    in1=factor.to_broadcast([P, count, ROPE // ROWS, ROWS]),
                     op=ALU.mult,
                 )
+            if (b + 1) % together == 0:
+                products[(n, b)] = products[n]
 
-        def store_query(n, b):
-            part = part_of(n)
-            if (b + 1) % part > 0:
+        def store(n, b):
+            if (n, b) not in products:
                 return
-            blocks = slice(b + 1 - part, b + 1)
+            blocks = slice(b + 1 - blocks_together(n), b + 1)
+            unit_0 = UNITS * n
+            unit_1 = UNITS * (n + 1)
             nc.sync.dma_start(
-                out=nope_out[:, blocks, ROPE * unrotated_before(UNITS * n) : ROPE * unrotated_before(UNITS * (n + 1))],
-                in_=nope_tiles[n][:, blocks, :, :].rearrange("p b s j -> p b (s j)"),
+                out=nope_out[:, blocks, ROPE * unrotated_before(unit_0) : ROPE * unrotated_before(unit_1)],
+                in_=unrotated[n][:, blocks, :, :].rearrange("p b u j -> p b (u j)"),
             )
-            straight, crossed = partial[(n, b // part)]
-            rotated = out_pool.tile(list(straight.shape), F32, name="rotated", tag="rotated")
+            straight, crossed = products[(n, b)]
+            rotated = rotated_pool.tile(list(straight.shape), F32, name="rotated", tag="rotated")
             for half, other in ((low, high), (high, low)):
                 nc.vector.tensor_tensor(
                     out=rotated[:, :, :, half], in0=straight[:, :, :, half], in1=crossed[:, :, :, other], op=ALU.add
                 )
             nc.sync.dma_start(
-                out=rope_out[:, blocks, ROPE * rotated_before(UNITS * n) : ROPE * rotated_before(UNITS * (n + 1))],
-                in_=rotated[:].rearrange("p b s j -> p b (s j)"),
+                out=rope_out[:, blocks, ROPE * rotated_before(unit_0) : ROPE * rotated_before(unit_1)],
+                in_=rotated[:].rearrange("p b u j -> p b (u j)"),
             )
 
-        a_items = []
-        singles = STEPS_A
-        b_items = [("b", n, g) for n in range(GROUPS_B) for g in range(PASSES_B)]
-        first, second = H_AT
-        steps = [[item] for item in singles]
-        for part in (b_items[0:first], [("h", 0, 0)], b_items[first:second], [("h", 1, 0)], b_items[second:]):
-            together = TOGETHER if part[0] == b_items[second] else 1
-            steps.extend([part[j : j + together] for j in range(0, len(part), together)])
-        place = {}
-        for i in range(len(steps)):
-            for item in steps[i]:
-                place[item] = i
+        a_items = [load + (passes,) for load in LOADS_A for passes in ((0, 1), (2, 3))]
+        b_items = [("b", n, 0, (g,)) for n in range(GROUPS_B) for g in range(PASSES_B)]
+        h_items = [("h", 0, half, tuple(range(PASSES_B))) for half in range(2)]
+        first, second = AHEAD_OF_H
+        items = a_items + b_items[:first] + h_items[:1] + b_items[first:second] + h_items[1:] + b_items[second:]
+        first_h = len(a_items) + first
 
-        products = []
-        for kind, n_groups, passes in (("a", GROUPS_A, PASSES_A), ("b", GROUPS_B, PASSES_B)):
-            for n in range(n_groups):
-                order = [(b, g) for b in range(TOKEN_BLOCKS) for g in range(passes)]
-                if (kind, n) == ("a", 0):
-                    order = [(b, g) for g in range(passes) for b in range(TOKEN_BLOCKS)]
-                products.extend([(kind, n, b, g, passes) for b, g in order])
+        complete = {}
+        for i in range(len(items)):
+            kind, n, half, passes = items[i]
+            for g in passes:
+                complete[(kind, half, g) if kind in "xh" else (kind, n, g)] = i
 
-        def needs(product):
-            kind, n, b, g, passes = product
-            act = ("x", 0, g) if kind == "a" else ("h", b // 2, 0)
-            return max(place[(kind, n, g)], place[act])
+        passes_left = [
+            (kind, n, b, g, passes)
+            for kind, groups, passes in (("a", GROUPS_A, PASSES_A), ("b", GROUPS_B, PASSES_B))
+            for n in range(groups)
+            for b in range(TOKEN_BLOCKS)
+            for g in range(passes)
+        ]
 
-        scaled_steps = 0
-        for i in range(AHEAD):
-            for item in steps[i]:
-                prescale(item)
-            scaled_steps += 1
+        def operands_complete(kind, n, b, g):
+            return max(complete[(kind, n, g)], complete[("x" if kind == "a" else "h", b // 2, g)])
+
+        for i in range(SCALE_AHEAD):
+            scale(items[i])
         closed = []
-        live = 0
-        done = 0
+        open_sums = 0
         i = 0
-        while done < len(products) or len(closed) > 0:
-            if i == SETUP_AT:
+        while len(passes_left) > 0 or len(closed) > 0:
+            if i == SETUP_STEP:
                 setup()
-            for what in FINISH:
-                if what == "T" and i < len(steps):
-                    for item in steps[i]:
-                        transposes(item)
-                    for item in steps[i]:
-                        copies_out(item)
-                if what == "V":
-                    for kind, n, b in closed:
-                        if (kind, n) != ("a", GROUPS_A - 1):
-                            (keep_latent if kind == "a" else multiply_rotated)(n, b)
-                if what == "S":
-                    for kind, n, b in closed:
-                        (sum_squares if kind == "a" else keep_unrotated)(n, b)
-            if 1 <= i <= len(steps):
-                for item in steps[i - 1]:
-                    quantises(item)
-            for what in TAIL:
-                if what == "P":
-                    while scaled_steps < len(steps) and scaled_steps <= i + AHEAD:
-                        for item in steps[scaled_steps]:
-                            prescale(item)
-                        scaled_steps += 1
-                for kind, n, b in closed:
-                    if what == "N" and (kind, n) == ("a", GROUPS_A - 1):
-                        normalise(b)
-                    if what == "S" and kind == "b":
-                        store_query(n, b)
-            live -= len(closed)
+            if i == len(a_items):
+                rotation_tables()
+            for kind, n, b in closed:
+                (sum_squares if kind == "a" else copy_unrotated)(n, b)
+            for kind, n, b in closed:
+                (keep_latent if kind == "a" else multiply_rotated)(n, b)
+            if i < len(items):
+                transpose(items[i])
+                empty(items[i])
+            if 1 <= i <= len(items):
+                quantise(items[i - 1])
+            for kind, n, b in closed:
+                if kind == "b":
+                    store(n, b)
+                elif n == GROUPS_A - 1:
+                    normalise(b)
+            if i + SCALE_AHEAD < len(items):
+                scale(items[i + SCALE_AHEAD])
+            open_sums -= len(closed)
             closed = []
-            budget = BUDGET_A if i < place[("h", 0, 0)] else BUDGET_B
-            slack = SLACK if i < len(steps) else 1
-            while done < len(products) and budget > 0 and needs(products[done]) <= i - slack:
-                kind, n, b, g, passes = products[done]
-                if g == 0 and live == ACCS:
+            behind = MULTIPLY_BEHIND if i < len(items) else 1
+            for turn in range(PASSES_A if i < first_h else 2 * PASSES_B):
+                if len(passes_left) == 0:
                     break
-                if g == 0:
-                    live += 1
+                kind, n, b, g, passes = passes_left[0]
+                if operands_complete(kind, n, b, g) > i - behind or (g == 0 and open_sums == SUM_BANKS):
+                    break
                 multiply(kind, n, b, g, passes)
+                passes_left = passes_left[1:]
+                if g == 0:
+                    open_sums += 1
                 if g == passes - 1:
                     closed.append((kind, n, b))
-                done += 1
-                budget -= 1
             i += 1

from contextlib import ExitStack

import concourse.masks as masks
import concourse.mybir as mybir

F32 = mybir.dt.float32
BF16 = mybir.dt.bfloat16
U32 = mybir.dt.uint32
U8 = mybir.dt.uint8
FP8X4 = mybir.dt.float8_e4m3fn_x4
ACT = mybir.ActivationFunctionType
ALU = mybir.AluOpType

P = 128
TOKENS = 512
HIDDEN = 2048
LATENT = 1536
HEADS = 16
NOPE = 128
ROPE = 64
HEAD = NOPE + ROPE
EPS = 1e-6

ROWS = 4
GROUP = ROWS * P
K_PASS = 4 * P
PASSES_A = HIDDEN // K_PASS
PASSES_B = LATENT // K_PASS
GROUPS_A = LATENT // GROUP
GROUPS_B = HEADS * HEAD // GROUP
TOKEN_BLOCKS = TOKENS // P
UNITS = GROUP // ROPE
FLOPS = 2 * TOKENS * HIDDEN * LATENT + 2 * TOKENS * LATENT * HEADS * HEAD

LOADS_A = (("a", 0, 0), ("a", 0, 1), ("x", 0, 0), ("a", 1, 0), ("x", 0, 1), ("a", 1, 1), ("a", 2, 0), ("a", 2, 1))
AHEAD_OF_H = (6, 7)
SCALE_AHEAD = 3
MULTIPLY_BEHIND = 3
SETUP_STEP = 4
SUM_BANKS = 4


def tile_deepseekv3attention_pa_kernel(
    tc, hidden_states, cos, sin, wq_a, sq_a, wq_b, sq_b, q_ln_w, out_0, out_1
):
    nc = tc.nc
    with ExitStack() as ctx:
        keep = ctx.enter_context(tc.tile_pool(name="keep", bufs=1))
        half_pool = ctx.enter_context(tc.tile_pool(name="half_pool", bufs=5))
        group_pool = ctx.enter_context(tc.tile_pool(name="group_pool", bufs=3))
        scaled_pool = ctx.enter_context(tc.tile_pool(name="scaled_pool", bufs=SCALE_AHEAD + 1))
        grouped_pool = ctx.enter_context(tc.tile_pool(name="grouped_pool", bufs=4))
        weight_pool = ctx.enter_context(tc.tile_pool(name="weight_pool", bufs=14))
        h_pool = ctx.enter_context(tc.tile_pool(name="h_pool", bufs=3))
        q_pool = ctx.enter_context(tc.tile_pool(name="q_pool", bufs=3))
        squares_pool = ctx.enter_context(tc.tile_pool(name="squares_pool", bufs=1))
        product_pool = ctx.enter_context(tc.tile_pool(name="product_pool", bufs=2))
        rotated_pool = ctx.enter_context(tc.tile_pool(name="rotated_pool", bufs=4))
        bank_pool = ctx.enter_context(tc.psum_pool(name="bank_pool", bufs=8 - SUM_BANKS))
        sum_pool = ctx.enter_context(tc.psum_pool(name="sum_pool", bufs=SUM_BANKS))
        ctx.enter_context(tc.manual_schedule())

        n_k_a = sq_a.shape[1]
        n_k_b = sq_b.shape[1]
        sq_rows = keep.tile([P, n_k_a + n_k_b], BF16)
        nc.vector.memset(sq_rows[:], 0.0)
        nc.sync.dma_start(out=sq_rows[0 : sq_a.shape[0], 0:n_k_a], in_=sq_a)
        nc.sync.dma_start(out=sq_rows[0 : sq_b.shape[0], n_k_a:], in_=sq_b)
        gain_row = h_pool.tile([P, LATENT], BF16, name="h_row", tag="h_row")
        nc.vector.memset(gain_row[:], 0.0)
        cos_bf = keep.tile([P, TOKEN_BLOCKS, ROPE], BF16)
        sin_bf = keep.tile([P, TOKEN_BLOCKS, ROPE], BF16)
        raw = {}

        def operand_rows(kind, n):
            if kind == "x":
                return hidden_states.rearrange("(b p) k -> p b k", p=P)
            weights = wq_a if kind == "a" else wq_b
            return weights[GROUP * n : GROUP * (n + 1), :].rearrange("(p r) k -> p r k", r=ROWS)

        def load_half(kind, n, half):
            tile = half_pool.tile([P, 2, HIDDEN], BF16, name="raw_half", tag="raw_half")
            nc.sync.dma_start(out=tile[:], in_=operand_rows(kind, n)[:, 2 * half : 2 * half + 2, :])
            raw[(kind, n, half)] = tile

        def load_group(n):
            tile = group_pool.tile([P, ROWS, LATENT], BF16, name="raw_group", tag="raw_group")
            nc.sync.dma_start(out=tile[:], in_=operand_rows("b", n))
            raw[("b", n, 0)] = tile

        for j in range(len(LOADS_A)):
            load_half(*LOADS_A[j])
            if j == 1:
                nc.sync.dma_start(out=gain_row[0:1, :], in_=q_ln_w.unsqueeze(0))
        nc.sync.dma_start(out=cos_bf[:], in_=cos.rearrange("(b p) j -> p b j", p=P))
        nc.sync.dma_start(out=sin_bf[:], in_=sin.rearrange("(b p) j -> p b j", p=P))
        groups_loaded = 3
        for n in range(groups_loaded):
            load_group(n)

        ident = keep.tile([P, P], F32)
        masks.make_identity(nc, ident[:])
        ones = keep.tile([P, P], BF16)
        nc.vector.memset(ones[:], 1.0)
        eps = keep.tile([P, 1], F32)
        nc.vector.memset(eps[:], EPS)
        first_sqrt = keep.tile([P, 1], F32)
        nc.scalar.activation(out=first_sqrt[:], in_=eps[:], func=ACT.Sqrt)

        select = keep.tile([P, GROUPS_B, P], BF16)
        nc.vector.tensor_copy(
            out=select[:].rearrange("b n (q i) -> b (n q) i", i=32),
            in_=ident[:, 0 : 4 * GROUPS_B].unsqueeze(2).to_broadcast([P, 4 * GROUPS_B, 32]),
        )
        factors = {}

        def factor_table(kind, groups, first, width):
            bank = bank_pool.tile([P, groups, width], F32, name="bank", tag="bank")
            for n in range(groups):
                nc.tensor.matmul(
                    out=bank[:, n, :],
                    lhsT=select[:, n, :],
                    rhs=sq_rows[:, first : first + width],
                    start=True,
                    stop=True,
                )
            factors[kind] = keep.tile([P, groups, width], F32, name="factors_" + kind)
            nc.scalar.copy(out=factors[kind][:], in_=bank[:])

        factor_table("a", GROUPS_A, 0, n_k_a)
        gain = keep.tile([P, LATENT], F32)

        def setup():
            factor_table("b", GROUPS_B, n_k_a, n_k_b)
            for n in range(GROUPS_A):
                cols = slice(GROUP * n, GROUP * (n + 1))
                bank = bank_pool.tile([P, GROUP], F32, name="bank", tag="bank")
                nc.tensor.matmul(out=bank[:], lhsT=ones[:], rhs=gain_row[:, cols], start=True, stop=True)
                nc.scalar.copy(out=gain[:, cols], in_=bank[:])

        low = slice(0, ROPE // 2)
        high = slice(ROPE // 2, ROPE)
        cos_sb = keep.tile([P, TOKEN_BLOCKS, ROPE], F32)
        sin_swapped = keep.tile([P, TOKEN_BLOCKS, ROPE], F32)

        def rotation_tables():
            nc.vector.tensor_copy(out=cos_sb[:], in_=cos_bf[:])
            nc.vector.tensor_copy(out=sin_swapped[:, :, low], in_=sin_bf[:, :, high])
            nc.vector.tensor_scalar_mul(out=sin_swapped[:, :, high], in0=sin_bf[:, :, low], scalar1=-1.0)

        item_rows = {}
        banks = {}
        grouped = {}
        codes = {}
        scales = {}
        x_codes = keep.tile([P, PASSES_A, TOKENS], U32, align_bytes=64)
        x_scales = keep.tile([P, PASSES_A, TOKENS], U8, align_bytes=64)
        h_codes = keep.tile([P, PASSES_B, TOKENS], U32, align_bytes=64)
        h_scales = keep.tile([P, PASSES_B, TOKENS], U8, align_bytes=64)
        h_rows = {}

        def scale(item):
            kind, n, half, passes = item
            if kind == "h":
                return
            source = raw[(kind, n, half)]
            first = K_PASS * passes[0]
            width = K_PASS * len(passes)
            if kind == "x":
                item_rows[item] = source[:, :, first : first + width]
                return
            scaled = scaled_pool.tile([P, source.shape[1], width], BF16, name="scaled", tag="scaled")
            for c in range(width // P):
                k_block = first // P + c
                nc.vector.tensor_scalar_mul(
                    out=scaled[:, :, P * c : P * (c + 1)],
                    in0=source[:, :, P * k_block : P * (k_block + 1)],
                    scalar1=factors[kind][:, n, k_block : k_block + 1],
                )
            item_rows[item] = scaled
            if kind == "b" and passes[-1] == PASSES_B - 1 and n + groups_loaded < GROUPS_B:
                load_group(n + groups_loaded)

        def transpose_pair(rows):
            bank = bank_pool.tile([P, 2, 2 * P], F32, name="bank", tag="bank")
            for u in range(2):
                for x in range(2):
                    words = rows[x].bitcast(F32)[:, P * u : P * (u + 1)]
                    nc.tensor.transpose(bank[:, u, P * x : P * (x + 1)], words, ident[:])
            return bank

        def transpose(item):
            kind, n, half, passes = item
            banks[item] = []
            for i in range(len(passes)):
                cols = slice(K_PASS * i, K_PASS * (i + 1))
                if kind == "h":
                    banks[item].append(transpose_pair([h_rows[2 * half + x][:, cols] for x in range(2)]))
                else:
                    rows = item_rows[item]
                    for pair in range(rows.shape[1] // 2):
                        banks[item].append(transpose_pair([rows[:, 2 * pair + x, cols] for x in range(2)]))

        def copy_out(some_banks):
            tile = grouped_pool.tile(
                [P, 2 * P * len(some_banks), 4], BF16, name="grouped", tag="grouped", align_bytes=64
            )
            for i in range(len(some_banks)):
                nc.scalar.copy(
                    out=tile[:, 2 * P * i : 2 * P * (i + 1), :].bitcast(F32),
                    in_=some_banks[i][:].rearrange("p u r -> p r u"),
                )
            return tile

        def empty(item):
            if item[0] == "h":
                grouped[item] = [copy_out([bank]) for bank in banks[item]]
            else:
                grouped[item] = [copy_out(banks[item])]

        def quantise_rows(rows, out, out_scales):
            nc.vector.quantize_mx(out=out.bitcast(FP8X4), scales=out_scales, in_=rows.rearrange("p r t -> p (r t)"))

        def quantise(item):
            kind, n, half, passes = item
            cols = slice(2 * P * half, 2 * P * (half + 1))
            if kind in "ab" and half == 0:
                for g in passes:
                    codes[(kind, n, g)] = weight_pool.tile(
                        [P, GROUP], U32, name="w_codes", tag="w_codes", align_bytes=64
                    )
                    scales[(kind, n, g)] = weight_pool.tile(
                        [P, GROUP], U8, name="w_scales", tag="w_scales", align_bytes=64
                    )
            if kind == "b":
                quantise_rows(grouped[item][0][:], codes[(kind, n, passes[0])][:], scales[(kind, n, passes[0])][:])
                return
            for i in range(len(passes)):
                g = passes[i]
                if kind == "h":
                    quantise_rows(grouped[item][i][:], h_codes[:, g, cols], h_scales[:, g, cols])
                else:
                    rows = grouped[item][0][:, 2 * P * i : 2 * P * (i + 1), :]
                    if kind == "x":
                        quantise_rows(rows, x_codes[:, g, cols], x_scales[:, g, cols])
                    else:
                        quantise_rows(rows, codes[(kind, n, g)][:, cols], scales[(kind, n, g)][:, cols])

        sums = {}

        def multiply(kind, n, b, g, passes):
            if g == 0:
                sums[(kind, n, b)] = sum_pool.tile([P, GROUP], F32, name="sum", tag="sum")
            act_codes, act_scales = (x_codes, x_scales) if kind == "a" else (h_codes, h_scales)
            tokens = slice(P * b, P * (b + 1))
            nc.tensor.matmul_mx(
                out=sums[(kind, n, b)][:],
                lhsT=act_codes[:, g, tokens].bitcast(FP8X4),
                lhsT_scale=act_scales[:, g, tokens],
                rhs=codes[(kind, n, g)][:].bitcast(FP8X4),
                rhs_scale=scales[(kind, n, g)][:],
                start=(g == 0),
                stop=(g == passes - 1),
            )

        latents = {}
        sum_sq = keep.tile([P, TOKEN_BLOCKS, GROUPS_A], F32)
        mean_sq = keep.tile([P, TOKEN_BLOCKS, GROUPS_A], F32)
        inv_rms = keep.tile([P, TOKEN_BLOCKS], F32)

        def in_row_order(columns):
            return columns.rearrange("t (r p) -> t p r", r=ROWS)

        def by_rows(columns):
            return columns.rearrange("t (p r) -> t p r", r=ROWS)

        def sum_squares(n, b):
            squares = squares_pool.tile([P, GROUP], BF16, name="squares", tag="squares")
            nc.scalar.activation(
                out=squares[:], in_=sums[("a", n, b)][:], func=ACT.Square, accum_out=sum_sq[:, b, n : n + 1]
            )
            nc.scalar.activation(
                out=mean_sq[:, b, n : n + 1],
                in_=sum_sq[:, b, n : n + 1],
                func=ACT.Sqrt if n == GROUPS_A - 1 else ACT.Identity,
                scale=1.0 / LATENT,
                bias=eps[:] if n == 0 else mean_sq[:, b, n - 1 : n],
            )

        def keep_latent(n, b):
            if n == GROUPS_A - 1:
                return
            cols = slice(GROUP * n, GROUP * (n + 1))
            if b == 0:
                latents[n] = q_pool.tile([P, TOKEN_BLOCKS, GROUP], F32, name="q_sb", tag="q_sb")
            nc.vector.tensor_tensor(
                out=by_rows(latents[n][:, b, :]),
                in0=in_row_order(sums[("a", n, b)][:]),
                in1=by_rows(gain[:, cols]),
                op=ALU.mult,
            )

        def normalise(b):
            one = slice(b, b + 1)
            nc.vector.reciprocal(out=inv_rms[:, one], in_=mean_sq[:, b, GROUPS_A - 1 : GROUPS_A])
            h_rows[b] = h_pool.tile([P, LATENT], BF16, name="h_row", tag="h_row")
            last = slice(GROUP * (GROUPS_A - 1), LATENT)
            nc.vector.scalar_tensor_tensor(
                out=by_rows(h_rows[b][:, last]),
                in0=in_row_order(sums[("a", GROUPS_A - 1, b)][:]),
                scalar=inv_rms[:, one],
                in1=by_rows(gain[:, last]),
                op0=ALU.mult,
                op1=ALU.mult,
            )
            for n in range(GROUPS_A - 1):
                nc.vector.tensor_scalar_mul(
                    out=h_rows[b][:, GROUP * n : GROUP * (n + 1)], in0=latents[n][:, b, :], scalar1=inv_rms[:, one]
                )

        nope_out = out_0.rearrange("(b p) h x -> p b (h x)", p=P)
        rope_out = out_1.rearrange("(b p) h j -> p b (h j)", p=P)
        unrotated = {}
        products = {}

        def unrotated_before(unit):
            return unit - unit // 3

        def rotated_before(unit):
            return unit // 3

        def blocks_together(n):
            return 1 if n == GROUPS_B - 1 else 2

        def units_of(n, b, remainder):
            first = (remainder - UNITS * n) % 3
            by_unit = sums[("b", n, b)][:].rearrange("t (r u q) -> t u q r", r=ROWS, u=UNITS)
            return by_unit[:, first:UNITS:3, :, :], first

        def copy_unrotated(n, b):
            unit_0 = UNITS * n
            if b == 0:
                width = unrotated_before(unit_0 + UNITS) - unrotated_before(unit_0)
                unrotated[n] = q_pool.tile([P, TOKEN_BLOCKS, width, ROPE], F32, name="q_sb", tag="q_sb")
            for remainder in range(2):
                columns, first = units_of(n, b, remainder)
                at = unrotated_before(unit_0 + first) - unrotated_before(unit_0)
                places = unrotated[n][:, b, at : at + 2 * columns.shape[1] - 1 : 2, :]
                nc.scalar.copy(out=places.rearrange("t u (q r) -> t u q r", r=ROWS), in_=columns)

        def multiply_rotated(n, b):
            together = blocks_together(n)
            columns, first = units_of(n, b, 2)
            count = columns.shape[1]
            if b % together == 0:
                products[n] = [
                    product_pool.tile([P, together, count, ROPE], F32, name=name, tag=name)
                    for name in ("straight", "crossed")
                ]
            for product, table in zip(products[n], (cos_sb, sin_swapped)):
                factor = table[:, b, :].rearrange("t (q r) -> t q r", r=ROWS).unsqueeze(1)
                nc.vector.tensor_tensor(
                    out=product[:, b % together, :, :].rearrange("t u (q r) -> t u q r", r=ROWS),
                    in0=columns,
                    in1=factor.to_broadcast([P, count, ROPE // ROWS, ROWS]),
                    op=ALU.mult,
                )
            if (b + 1) % together == 0:
                products[(n, b)] = products[n]

        def store(n, b):
            if (n, b) not in products:
                return
            blocks = slice(b + 1 - blocks_together(n), b + 1)
            unit_0 = UNITS * n
            unit_1 = UNITS * (n + 1)
            nc.sync.dma_start(
                out=nope_out[:, blocks, ROPE * unrotated_before(unit_0) : ROPE * unrotated_before(unit_1)],
                in_=unrotated[n][:, blocks, :, :].rearrange("p b u j -> p b (u j)"),
            )
            straight, crossed = products[(n, b)]
            rotated = rotated_pool.tile(list(straight.shape), F32, name="rotated", tag="rotated")
            for half, other in ((low, high), (high, low)):
                nc.vector.tensor_tensor(
                    out=rotated[:, :, :, half], in0=straight[:, :, :, half], in1=crossed[:, :, :, other], op=ALU.add
                )
            nc.sync.dma_start(
                out=rope_out[:, blocks, ROPE * rotated_before(unit_0) : ROPE * rotated_before(unit_1)],
                in_=rotated[:].rearrange("p b u j -> p b (u j)"),
            )

        a_items = [load + (passes,) for load in LOADS_A for passes in ((0, 1), (2, 3))]
        b_items = [("b", n, 0, (g,)) for n in range(GROUPS_B) for g in range(PASSES_B)]
        h_items = [("h", 0, half, tuple(range(PASSES_B))) for half in range(2)]
        first, second = AHEAD_OF_H
        items = a_items + b_items[:first] + h_items[:1] + b_items[first:second] + h_items[1:] + b_items[second:]
        first_h = len(a_items) + first

        complete = {}
        for i in range(len(items)):
            kind, n, half, passes = items[i]
            for g in passes:
                complete[(kind, half, g) if kind in "xh" else (kind, n, g)] = i

        passes_left = [
            (kind, n, b, g, passes)
            for kind, groups, passes in (("a", GROUPS_A, PASSES_A), ("b", GROUPS_B, PASSES_B))
            for n in range(groups)
            for b in range(TOKEN_BLOCKS)
            for g in range(passes)
        ]

        def operands_complete(kind, n, b, g):
            return max(complete[(kind, n, g)], complete[("x" if kind == "a" else "h", b // 2, g)])

        for i in range(SCALE_AHEAD):
            scale(items[i])
        closed = []
        open_sums = 0
        i = 0
        while len(passes_left) > 0 or len(closed) > 0:
            if i == SETUP_STEP:
                setup()
            if i == len(a_items):
                rotation_tables()
            for kind, n, b in closed:
                (sum_squares if kind == "a" else copy_unrotated)(n, b)
            for kind, n, b in closed:
                (keep_latent if kind == "a" else multiply_rotated)(n, b)
            if i < len(items):
                transpose(items[i])
                empty(items[i])
            if 1 <= i <= len(items):
                quantise(items[i - 1])
            for kind, n, b in closed:
                if kind == "b":
                    store(n, b)
                elif n == GROUPS_A - 1:
                    normalise(b)
            if i + SCALE_AHEAD < len(items):
                scale(items[i + SCALE_AHEAD])
            open_sums -= len(closed)
            closed = []
            behind = MULTIPLY_BEHIND if i < len(items) else 1
            for turn in range(PASSES_A if i < first_h else 2 * PASSES_B):
                if len(passes_left) == 0:
                    break
                kind, n, b, g, passes = passes_left[0]
                if operands_complete(kind, n, b, g) > i - behind or (g == 0 and open_sums == SUM_BANKS):
                    break
                multiply(kind, n, b, g, passes)
                passes_left = passes_left[1:]
                if g == 0:
                    open_sums += 1
                if g == passes - 1:
                    closed.append((kind, n, b))
            i += 1
